import numpy as np
import ml_dtypes


def mxq(x, axis, fmt="e4m3"):
    dtype, down = {"e4m3": (ml_dtypes.float8_e4m3fn, 7), "e5m2": (ml_dtypes.float8_e5m2, 14)}[fmt]
    v = np.moveaxis(np.asarray(x, np.float32).astype(ml_dtypes.bfloat16).astype(np.float64), axis, -1)
    blocks = v.reshape(v.shape[:-1] + (-1, 32))
    amax = np.abs(blocks).max(-1, keepdims=True)
    byte = np.maximum(np.where(amax > 0, np.frexp(amax)[1] - 1 + 127, 0) - down, 1)
    scale = np.exp2(byte - 127.0)
    codes = (blocks / scale).astype(np.float32).astype(dtype).astype(np.float64)
    return np.moveaxis((codes * scale).reshape(v.shape), -1, axis)


WIDE = False


def mx_kscale(k):
    if not WIDE:
        return np.ones(k)
    levels = np.array([10, -10, 5, -5, 0])
    if k % 512:
        return np.exp2(np.random.permutation(np.resize(levels, k // 32))).repeat(32)
    a = np.empty((k // 512, 16))
    for p in range(k // 512):
        a[p, :8] = np.random.permutation(np.resize(levels, 8))
        for g in range(8):
            far = levels[np.abs(levels - a[p, g]) >= 10]
            a[p, g + 8] = far[np.random.randint(len(far))]
    return np.exp2(a.ravel()).repeat(32)


BF16 = ml_dtypes.bfloat16


def bf(x):
    return np.asarray(x, np.float32).astype(BF16)


def f64(x):
    return np.asarray(x).astype(np.float64)


B, N, P, D, H = 8, 512, 4, 128, 2
E = P * D
DH = E // H


def sincos_table(n, e):
    pe = np.zeros((n, e))
    position = np.arange(n, dtype=np.float64)[:, None]
    div_term = np.exp(np.arange(0, e, 2, dtype=np.float64) * -(np.log(10000.0) / e))
    pe[:, 0::2] = np.sin(position * div_term)
    pe[:, 1::2] = np.cos(position * div_term)
    pe = pe - pe.mean()
    return pe / (pe.std() * 10)


def setup_inputs():
    s, t = mx_kscale(E), mx_kscale(E)
    c = 1.0 / np.sqrt(E)
    return {"x": bf(np.random.standard_normal((B, N, P, D)) * s.reshape(P, D)),
            "pos_embed": bf(sincos_table(N, E) * t),
            "W_embed": bf(np.random.standard_normal((E, E)) * c * t[:, None] / s),
            "b_embed": bf(np.random.standard_normal(E) * 0.1 * t),
            "Wq": bf(np.random.standard_normal((E, E)) * c / t),
            "bq": bf(np.random.standard_normal(E) * 0.1),
            "Wk": bf(np.random.standard_normal((E, E)) * c / t),
            "bk": bf(np.random.standard_normal(E) * 0.1),
            "Wv": bf(np.random.standard_normal((E, E)) * c / t),
            "bv": bf(np.random.standard_normal(E) * 0.1)}


def reference(x, pos_embed, W_embed, b_embed, Wq, bq, Wk, bk, Wv, bv):
    xf = f64(x).reshape(B, N, E)
    xe = (mxq(xf, 2, "e4m3") @ mxq(f64(W_embed).T, 0, "e4m3")) + f64(b_embed)
    xe = xe + f64(pos_embed)
    xq = mxq(xe, 2, "e4m3")
    q = ((xq @ mxq(f64(Wq).T, 0, "e4m3")) + f64(bq)).reshape(B, N, H, DH)
    k = ((xq @ mxq(f64(Wk).T, 0, "e4m3")) + f64(bk)).reshape(B, N, H, DH)
    v = ((xq @ mxq(f64(Wv).T, 0, "e4m3")) + f64(bv)).reshape(B, N, H, DH)
    return q, k, v

@@ -1,0 +1,376 @@
+from contextlib import ExitStack
+
+import concourse.mybir as mybir
+from concourse.masks import make_identity
+
+F32 = mybir.dt.float32
+BF16 = mybir.dt.bfloat16
+U32 = mybir.dt.uint32
+U8 = mybir.dt.uint8
+I32 = mybir.dt.int32
+FP8X4 = mybir.dt.float8_e4m3fn_x4
+ADD = mybir.AluOpType.add
+IDENTITY = mybir.ActivationFunctionType.Identity
+
+P = 128
+E = 512
+H = E // 2
+GROUPS = 8
+SLABS = 4
+Q, K, V = 0, 1, 2
+
+FLOPS = 2 * GROUPS * SLABS * P * E * E * 4
+
+
+def tile_attention_pa_t_kernel(
+    tc, x, pos_embed, W_embed, b_embed, Wq, bq, Wk, bk, Wv, bv, out_0, out_1, out_2
+):
+    nc = tc.nc
+    outs = [out_0, out_1, out_2]
+    weights = [Wq, Wk, Wv]
+    biases = [bq, bk, bv]
+    with ExitStack() as ctx:
+        consts = ctx.enter_context(tc.tile_pool(name="consts", bufs=1))
+        raws = ctx.enter_context(tc.tile_pool(name="raws", bufs=1))
+        work = ctx.enter_context(tc.tile_pool(name="work", bufs=2))
+        stage = ctx.enter_context(tc.tile_pool(name="stage", bufs=4))
+        prep_pool = ctx.enter_context(tc.psum_pool(name="prep", bufs=4))
+        s2_pool = ctx.enter_context(tc.psum_pool(name="s2", bufs=3))
+        vlow_pool = ctx.enter_context(tc.psum_pool(name="vlow", bufs=1))
+        ctx.enter_context(tc.manual_schedule())
+
+        def bank_of(pool, tag):
+            return pool.tile([P, E], F32, tag=tag, name="bank_" + tag)
+
+        ident = consts.tile([P, P], F32)
+        make_identity(nc, ident[:])
+        be_rows = consts.tile([P, E], BF16)
+        nc.vector.memset(be_rows[:].bitcast(I32), 0)
+        ones = consts.tile([P, P], BF16)
+        nc.vector.memset(ones[:], 1.0)
+        bias_rows = consts.tile([P, 3 * E], BF16)
+        nc.vector.memset(bias_rows[:].bitcast(I32), 0)
+        warm = consts.tile([P, 1], F32)
+        nc.scalar.activation(out=warm[:], in_=ones[:, 0:1], func=IDENTITY)
+
+        we_raw = raws.tile([P, 4 * E], BF16)
+        we_view = W_embed.rearrange("(m t) k -> m (t k)", t=4)
+        x_raw = [raws.tile([P, 4 * E], BF16, name="x_raw%d" % g) for g in range(GROUPS)]
+        x_views = [x[g].rearrange("(c j) a d -> c (j a d)", j=SLABS) for g in range(GROUPS)]
+        pos_raw = raws.tile([P, 4 * E], BF16)
+        pos_view = pos_embed.rearrange("(c j) e -> c (j e)", j=SLABS)
+        w_raw = [raws.tile([P, 4 * E], BF16, name="w_raw%d" % o) for o in range(3)]
+        for half in range(2):
+            cols = slice(2 * E * half, 2 * E * (half + 1))
+            nc.sync.dma_start(out=we_raw[:, cols], in_=we_view[:, cols])
+        nc.sync.dma_start(out=be_rows[0:1, :], in_=b_embed.rearrange("(o n) -> o n", o=1))
+        for dst, view in ((x_raw[0], x_views[0]), (pos_raw, pos_view)):
+            for half in range(2):
+                cols = slice(2 * E * half, 2 * E * (half + 1))
+                nc.sync.dma_start(out=dst[:, cols], in_=view[:, cols])
+        for o in (K, Q, V):
+            nc.sync.dma_start(
+                out=w_raw[o][:], in_=weights[o].rearrange("(m s) k -> m (s k)", s=SLABS)
+            )
+            nc.sync.dma_start(
+                out=bias_rows[0:1, E * o : E * (o + 1)],
+                in_=biases[o].rearrange("(o n) -> o n", o=1),
+            )
+        for g in range(1, GROUPS):
+            nc.sync.dma_start(out=x_raw[g][:], in_=x_views[g])
+
+        we_mx = (
+            consts.tile([P, E], U32, align_bytes=64, name="we_codes"),
+            consts.tile([P, E], U8, align_bytes=64, name="we_scales"),
+        )
+        w_mx = [
+            (
+                consts.tile([P, E], U32, align_bytes=64, name="w_codes%d" % o),
+                consts.tile([P, E], U8, align_bytes=64, name="w_scales%d" % o),
+            )
+            for o in range(3)
+        ]
+        bias_all = consts.tile([P, 3 * E], F32)
+        be_col = consts.tile([P, 4], F32)
+        bv_col = consts.tile([P, 2], F32)
+        pos_t = consts.tile([P, 4 * E], F32)
+
+        grouped_x = {}
+        x_mx = {}
+        grouped_xe = {}
+        xe_mx = {}
+        banks = {}
+        staged = {}
+        v_high = {}
+
+        def new_grouped():
+            grouped = work.tile([P, 4 * E], BF16, align_bytes=64, tag="grouped", bufs=4)
+            return grouped
+
+        def new_mx(tag):
+            return (
+                work.tile([P, E], U32, align_bytes=64, tag=tag + "_codes", name=tag + "_codes"),
+                work.tile([P, E], U8, align_bytes=64, tag=tag + "_scales", name=tag + "_scales"),
+            )
+
+        def turn_words(raw, half, pool, tag):
+            words = raw[:].bitcast(F32)
+            bank = bank_of(pool, tag)
+            for s in range(2):
+                start = H * (2 * half + s)
+                for u in range(2):
+                    nc.tensor.transpose(
+                        bank[:, block(2 * s + u)], words[:, start + u : start + H : 2], ident[:]
+                    )
+            return bank
+
+        def turn_half(raw, grouped, half, rows_interleaved, copy):
+            bank = turn_words(raw, half, prep_pool, "prep")
+            gwords = grouped[:].bitcast(F32)
+            if rows_interleaved:
+                copy(
+                    out=gwords.rearrange("p (m s u) -> p m s u", s=4, u=2)[
+                        :, :, 2 * half : 2 * half + 2, :
+                    ],
+                    in_=bank[:].rearrange("p (s u m) -> p m s u", s=2, u=2),
+                )
+            else:
+                copy(
+                    out=gwords.rearrange("p (s m u) -> p s m u", s=4, u=2)[
+                        :, 2 * half : 2 * half + 2, :, :
+                    ],
+                    in_=bank[:].rearrange("p (s u m) -> p s m u", s=2, u=2),
+                )
+
+        def turn_x(g):
+            grouped_x[g] = new_grouped()
+            for half in range(2):
+                turn_half(x_raw[g], grouped_x[g], half, False, nc.scalar.copy)
+
+        def quantise(grouped, mx):
+            nc.vector.quantize_mx(out=mx[0][:].bitcast(FP8X4), scales=mx[1][:], in_=grouped[:])
+
+        def quantise_x(g):
+            x_mx[g] = new_mx("x")
+            quantise(grouped_x[g], x_mx[g])
+
+        def quantise_xe(g):
+            xe_mx[g] = new_mx("xe")
+            quantise(grouped_xe[g], xe_mx[g])
+
+        def mx_pass(out, stationary, s_cols, moving, m_cols):
+            nc.tensor.matmul_mx(
+                out=out,
+                lhsT=stationary[0][:, s_cols].bitcast(FP8X4),
+                lhsT_scale=stationary[1][:, s_cols],
+                rhs=moving[0][:, m_cols].bitcast(FP8X4),
+                rhs_scale=moving[1][:, m_cols],
+                start=True,
+                stop=True,
+            )
+
+        def block(i):
+            return slice(P * i, P * (i + 1))
+
+        def stage1_passes(g, j, pool, tag):
+            bank = bank_of(pool, tag)
+            for t in range(4):
+                mx_pass(bank[:, block(t)], we_mx, block(t), x_mx[g], block(j))
+            banks[("s1", j)] = bank
+
+        def stage1_exit(g, j):
+            if j == 0:
+                grouped_xe[g] = work.tile([P, 4 * E], BF16, align_bytes=64, tag="xe", name="xe")
+            cols = slice(E * j, E * (j + 1))
+            nc.vector.tensor_tensor(
+                out=grouped_xe[g][:, cols].rearrange("p (c t) -> p c t", t=4),
+                in0=banks[("s1", j)][:].rearrange("p (t c) -> p c t", t=4),
+                in1=pos_t[:, cols].rearrange("p (c t) -> p c t", t=4),
+                op=ADD,
+            )
+
+        def staged_slab(o, j):
+            if j % 2 == 0:
+                staged[(o, j // 2)] = stage.tile([P, 2 * E], F32, name="st%d" % o, tag="st%d" % o)
+            return staged[(o, j // 2)][:, E * (j % 2) : E * (j % 2 + 1)]
+
+        def full_pass(g, j, o):
+            banks[o] = bank_of(s2_pool, "s2")
+            mx_pass(banks[o][:], xe_mx[g], block(j), w_mx[o], slice(0, E))
+
+        def q_exit(j):
+            nc.vector.tensor_tensor(
+                out=staged_slab(Q, j), in0=banks[Q][:], in1=bias_all[:, E * Q : E * (Q + 1)], op=ADD
+            )
+
+        def k_exit(j):
+            slab = staged_slab(K, j)
+            nc.scalar.copy(out=slab, in_=banks[K][:])
+            nc.gpsimd.tensor_tensor(
+                out=slab, in0=slab, in1=bias_all[:, E * K : E * (K + 1)], op=ADD
+            )
+
+        def v_low_pass(g, j):
+            if j % 2 == 0:
+                banks[V] = bank_of(vlow_pool, "vlow")
+                staged[(V, j // 2)] = stage.tile([P, 2 * E], F32, name="st2", tag="st2")
+            mx_pass(
+                banks[V][:, H * (j % 2) : H * (j % 2 + 1)], xe_mx[g], block(j), w_mx[V], slice(0, H)
+            )
+
+        def v_low_exit(pair):
+            nc.vector.tensor_tensor(
+                out=staged[(V, pair)][:].rearrange("c (j e) -> c j e", j=2)[:, :, 0:H],
+                in0=banks[V][:].rearrange("c (j e) -> c j e", j=2),
+                in1=bias_all[:, E * V : E * V + H].unsqueeze(1).to_broadcast([P, 2, H]),
+                op=ADD,
+            )
+
+        def v_high_pass(g, i):
+            banks[("vh", i)] = bank_of(s2_pool, "s2")
+            mx_pass(banks[("vh", i)][:], w_mx[V], slice(H + P * i, H + P * (i + 1)), xe_mx[g], slice(0, E))
+
+        def v_high_bias(i):
+            v_high[i] = work.tile([P, E], F32, tag="v_high", name="v_high", bufs=4)
+            nc.scalar.activation(
+                out=v_high[i][:], in_=banks[("vh", i)][:], func=IDENTITY, bias=bv_col[:, i : i + 1]
+            )
+
+        def v_high_back(pair):
+            bank = bank_of(prep_pool, "prep")
+            for j2 in range(2):
+                for i in range(2):
+                    nc.tensor.transpose(
+                        bank[:, block(2 * j2 + i)], v_high[i][:, block(2 * pair + j2)], ident[:]
+                    )
+            nc.scalar.copy(
+                out=staged[(V, pair)][:].rearrange("c (j e) -> c j e", j=2)[:, :, H:E],
+                in_=bank[:].rearrange("c (j e) -> c j e", j=2),
+            )
+
+        def store(g, o, pair):
+            nc.sync.dma_start(
+                out=outs[o][g].rearrange("(c j) h d -> c (j h d)", j=SLABS)[
+                    :, 2 * E * pair : 2 * E * (pair + 1)
+                ],
+                in_=staged[(o, pair)][:],
+            )
+
+        grouped_we = new_grouped()
+        turn_half(we_raw, grouped_we, 0, False, nc.vector.tensor_copy)
+        turn_half(we_raw, grouped_we, 1, False, nc.scalar.copy)
+        turn_x(0)
+        be_bank = bank_of(s2_pool, "s2")
+        for u in range(2):
+            nc.tensor.transpose(be_bank[:, block(u)], be_rows[:].bitcast(F32)[:, u:H:2], ident[:])
+        nc.scalar.copy(
+            out=be_col[:].rearrange("p (u e) -> p u e", u=2),
+            in_=be_bank[:].bitcast(BF16).rearrange("p (u w) -> p u w", u=4)[:, 0:2, 0:2],
+        )
+        pos_banks = [turn_words(pos_raw, 0, s2_pool, "s2"), turn_words(pos_raw, 1, vlow_pool, "vlow")]
+        quantise(grouped_we, we_mx)
+        quantise_x(0)
+        grouped_w = {}
+
+        def turn_weight(o):
+            grouped_w[o] = new_grouped()
+            for half in range(2):
+                turn_half(w_raw[o], grouped_w[o], half, True, nc.scalar.copy)
+
+        def spread_bias(o):
+            bank = bank_of(s2_pool, "s2")
+            cols = slice(E * o, E * (o + 1))
+            nc.tensor.matmul(out=bank[:], lhsT=ones[:], rhs=bias_rows[:, cols], start=True, stop=True)
+            nc.scalar.copy(out=bias_all[:, cols], in_=bank[:])
+
+        turn_weight(K)
+        for j in range(SLABS):
+            if j < 2:
+                stage1_passes(0, j, prep_pool, "prep")
+            else:
+                stage1_passes(0, j, s2_pool, "s2")
+        for j in range(SLABS):
+            nc.vector.tensor_tensor(
+                out=pos_t[:, E * j : E * (j + 1)].rearrange("p (c u e) -> p c u e", u=2, e=2),
+                in0=pos_banks[j // 2][:]
+                .bitcast(BF16)
+                .rearrange("p (s u c e) -> p s c u e", s=2, u=2, e=2)[:, j % 2],
+                in1=be_col[:].rearrange("p (o u e) -> p o u e", o=1, u=2).to_broadcast([P, P, 2, 2]),
+                op=ADD,
+            )
+        for j in range(SLABS):
+            stage1_exit(0, j)
+        turn_weight(Q)
+        turn_x(1)
+        turn_weight(V)
+        for o in (V, Q, K):
+            spread_bias(o)
+        quantise(grouped_w[K], w_mx[K])
+        quantise(grouped_w[Q], w_mx[Q])
+        quantise_xe(0)
+        quantise_x(1)
+        quantise(grouped_w[V], w_mx[V])
+        for j in range(2):
+            stage1_passes(1, j, prep_pool, "prep")
+        bv_bank = bank_of(s2_pool, "s2")
+        for i in range(2):
+            nc.tensor.transpose(
+                bv_bank[:, block(i)], bias_all[:, E * V + H + P * i : E * V + H + P * (i + 1)], ident[:]
+            )
+        nc.scalar.copy(
+            out=bv_col[:].unsqueeze(2),
+            in_=bv_bank[:].rearrange("p (i c) -> p i c", c=P)[:, 0:2, 0:1],
+        )
+        for j in range(2):
+            stage1_exit(1, j)
+
+        for g in range(GROUPS):
+            for j in range(SLABS):
+                for o in (K, Q) if j == 0 else (Q, K):
+                    full_pass(g, j, o)
+                v_low_pass(g, j)
+                if j == 0:
+                    v_high_pass(g, 0)
+                    v_high_pass(g, 1)
+                if j == 0:
+                    k_exit(j)
+                    q_exit(j)
+                elif j < 3:
+                    q_exit(j)
+                    k_exit(j)
+                else:
+                    k_exit(j)
+                if j == 0:
+                    v_high_bias(0)
+                    v_high_bias(1)
+                    if g + 1 < GROUPS:
+                        stage1_passes(g + 1, 2, prep_pool, "prep")
+                        stage1_passes(g + 1, 3, prep_pool, "prep")
+                        stage1_exit(g + 1, 2)
+                        stage1_exit(g + 1, 3)
+                if j == 1:
+                    v_low_exit(0)
+                    if g + 2 < GROUPS:
+                        turn_x(g + 2)
+                    store(g, Q, 0)
+                if j == 2:
+                    v_high_back(0)
+                    v_high_back(1)
+                if j == 3:
+                    store(g, K, 0)
+                    store(g, V, 0)
+                    if g + 2 < GROUPS:
+                        quantise_x(g + 2)
+                    if g + 1 < GROUPS:
+                        quantise_xe(g + 1)
+                    if g + 2 < GROUPS:
+                        stage1_passes(g + 2, 0, prep_pool, "prep")
+                        stage1_passes(g + 2, 1, prep_pool, "prep")
+                    q_exit(j)
+                    v_low_exit(1)
+                    if g + 2 < GROUPS:
+                        stage1_exit(g + 2, 0)
+                        stage1_exit(g + 2, 1)
+                    store(g, Q, 1)
+                    store(g, V, 1)
+                    store(g, K, 1)

@@ -79,25 +79,20 @@ def tile_attention_pa_t_kernel(
         for g in range(1, GROUPS):
             nc.sync.dma_start(out=x_raw[g][:], in_=x_views[g])
 
-        we_mx = (
-            consts.tile([P, E], U32, align_bytes=64, name="we_codes"),
-            consts.tile([P, E], U8, align_bytes=64, name="we_scales"),
-        )
-        w_mx = [
-            (
-                consts.tile([P, E], U32, align_bytes=64, name="w_codes%d" % o),
-                consts.tile([P, E], U8, align_bytes=64, name="w_scales%d" % o),
-            )
-            for o in range(3)
-        ]
+        def weight_mx(name):
+            codes = consts.tile([P, E], U32, align_bytes=64, name=name + "_codes")
+            scales = consts.tile([P, E], U8, align_bytes=64, name=name + "_scales")
+            return (codes[:], scales[:])
+
+        we_mx = weight_mx("we")
+        w_mx = [weight_mx("w%d" % o) for o in range(3)]
         bias_all = consts.tile([P, 3 * E], F32)
         be_col = consts.tile([P, 4], F32)
         bv_col = consts.tile([P, 2], F32)
         pos_t = consts.tile([P, 4 * E], F32)
 
-        grouped_x = {}
+        pairs = {}
         x_mx = {}
-        grouped_xe = {}
         xe_mx = {}
         banks = {}
         staged = {}
@@ -107,11 +102,10 @@ def tile_attention_pa_t_kernel(
             grouped = work.tile([P, 4 * E], BF16, align_bytes=64, tag="grouped", bufs=4)
             return grouped
 
-        def new_mx(tag):
-            return (
-                work.tile([P, E], U32, align_bytes=64, tag=tag + "_codes", name=tag + "_codes"),
-                work.tile([P, E], U8, align_bytes=64, tag=tag + "_scales", name=tag + "_scales"),
-            )
+        def pair_of(n):
+            if n not in pairs:
+                pairs[n] = work.tile([P, 8 * E], BF16, align_bytes=64, tag="pair", name="pair")
+            return pairs[n]
 
         def turn_words(raw, half, pool, tag):
             words = raw[:].bitcast(F32)
@@ -126,7 +120,7 @@ def tile_attention_pa_t_kernel(
 
         def turn_half(raw, grouped, half, rows_interleaved, copy):
             bank = turn_words(raw, half, prep_pool, "prep")
-            gwords = grouped[:].bitcast(F32)
+            gwords = grouped.bitcast(F32)
             if rows_interleaved:
                 copy(
                     out=gwords.rearrange("p (m s u) -> p m s u", s=4, u=2)[
@@ -143,20 +137,22 @@ def tile_attention_pa_t_kernel(
                 )
 
         def turn_x(g):
-            grouped_x[g] = new_grouped()
             for half in range(2):
-                turn_half(x_raw[g], grouped_x[g], half, False, nc.scalar.copy)
+                turn_half(x_raw[g], pair_of(g - 1)[:, 4 * E : 8 * E], half, False, nc.scalar.copy)
 
         def quantise(grouped, mx):
-            nc.vector.quantize_mx(out=mx[0][:].bitcast(FP8X4), scales=mx[1][:], in_=grouped[:])
+            nc.vector.quantize_mx(out=mx[0].bitcast(FP8X4), scales=mx[1], in_=grouped)
 
-        def quantise_x(g):
-            x_mx[g] = new_mx("x")
-            quantise(grouped_x[g], x_mx[g])
-
-        def quantise_xe(g):
-            xe_mx[g] = new_mx("xe")
-            quantise(grouped_xe[g], xe_mx[g])
+        def quantise_pair(n):
+            codes = work.tile([P, 2 * E], U32, align_bytes=64, tag="codes", name="codes")
+            scales = work.tile([P, 2 * E], U8, align_bytes=64, tag="scales", name="scales")
+            first = 0 if n >= 0 else E
+            last = 2 * E if n + 1 < GROUPS else E
+            quantise(
+                pair_of(n)[:, 4 * first : 4 * last], (codes[:, first:last], scales[:, first:last])
+            )
+            xe_mx[n] = (codes[:, 0:E], scales[:, 0:E])
+            x_mx[n + 1] = (codes[:, E : 2 * E], scales[:, E : 2 * E])
 
         def mx_pass(out, stationary, s_cols, moving, m_cols):
             nc.tensor.matmul_mx(
@@ -179,11 +175,9 @@ def tile_attention_pa_t_kernel(
             banks[("s1", j)] = bank
 
         def stage1_exit(g, j):
-            if j == 0:
-                grouped_xe[g] = work.tile([P, 4 * E], BF16, align_bytes=64, tag="xe", name="xe")
             cols = slice(E * j, E * (j + 1))
             nc.vector.tensor_tensor(
-                out=grouped_xe[g][:, cols].rearrange("p (c t) -> p c t", t=4),
+                out=pair_of(g)[:, cols].rearrange("p (c t) -> p c t", t=4),
                 in0=banks[("s1", j)][:].rearrange("p (t c) -> p c t", t=4),
                 in1=pos_t[:, cols].rearrange("p (c t) -> p c t", t=4),
                 op=ADD,
@@ -257,8 +251,8 @@ def tile_attention_pa_t_kernel(
             )
 
         grouped_we = new_grouped()
-        turn_half(we_raw, grouped_we, 0, False, nc.vector.tensor_copy)
-        turn_half(we_raw, grouped_we, 1, False, nc.scalar.copy)
+        turn_half(we_raw, grouped_we[:], 0, False, nc.vector.tensor_copy)
+        turn_half(we_raw, grouped_we[:], 1, False, nc.scalar.copy)
         turn_x(0)
         be_bank = bank_of(s2_pool, "s2")
         for u in range(2):
@@ -268,14 +262,14 @@ def tile_attention_pa_t_kernel(
             in_=be_bank[:].bitcast(BF16).rearrange("p (u w) -> p u w", u=4)[:, 0:2, 0:2],
         )
         pos_banks = [turn_words(pos_raw, 0, s2_pool, "s2"), turn_words(pos_raw, 1, vlow_pool, "vlow")]
-        quantise(grouped_we, we_mx)
-        quantise_x(0)
+        quantise(grouped_we[:], we_mx)
+        quantise_pair(-1)
         grouped_w = {}
 
         def turn_weight(o):
             grouped_w[o] = new_grouped()
             for half in range(2):
-                turn_half(w_raw[o], grouped_w[o], half, True, nc.scalar.copy)
+                turn_half(w_raw[o], grouped_w[o][:], half, True, nc.scalar.copy)
 
         def spread_bias(o):
             bank = bank_of(s2_pool, "s2")
@@ -305,11 +299,10 @@ def tile_attention_pa_t_kernel(
         turn_weight(V)
         for o in (V, Q, K):
             spread_bias(o)
-        quantise(grouped_w[K], w_mx[K])
-        quantise(grouped_w[Q], w_mx[Q])
-        quantise_xe(0)
-        quantise_x(1)
-        quantise(grouped_w[V], w_mx[V])
+        quantise(grouped_w[K][:], w_mx[K])
+        quantise(grouped_w[Q][:], w_mx[Q])
+        quantise_pair(0)
+        quantise(grouped_w[V][:], w_mx[V])
         for j in range(2):
             stage1_passes(1, j, prep_pool, "prep")
         bv_bank = bank_of(s2_pool, "s2")
@@ -359,10 +352,8 @@ def tile_attention_pa_t_kernel(
                 if j == 3:
                     store(g, K, 0)
                     store(g, V, 0)
-                    if g + 2 < GROUPS:
-                        quantise_x(g + 2)
                     if g + 1 < GROUPS:
-                        quantise_xe(g + 1)
+                        quantise_pair(g + 1)
                     if g + 2 < GROUPS:
                         stage1_passes(g + 2, 0, prep_pool, "prep")
                         stage1_passes(g + 2, 1, prep_pool, "prep")

@@ -34,13 +34,11 @@ def tile_attention_pa_t_kernel(
         raws = ctx.enter_context(tc.tile_pool(name="raws", bufs=1))
         work = ctx.enter_context(tc.tile_pool(name="work", bufs=2))
         stage = ctx.enter_context(tc.tile_pool(name="stage", bufs=4))
-        prep_pool = ctx.enter_context(tc.psum_pool(name="prep", bufs=4))
-        s2_pool = ctx.enter_context(tc.psum_pool(name="s2", bufs=3))
-        vlow_pool = ctx.enter_context(tc.psum_pool(name="vlow", bufs=1))
+        bank_pool = ctx.enter_context(tc.psum_pool(name="banks", bufs=8))
         ctx.enter_context(tc.manual_schedule())
 
-        def bank_of(pool, tag):
-            return pool.tile([P, E], F32, tag=tag, name="bank_" + tag)
+        def new_bank():
+            return bank_pool.tile([P, E], F32, tag="bank", name="bank")
 
         ident = consts.tile([P, P], F32)
         make_identity(nc, ident[:])
@@ -69,6 +67,8 @@ def tile_attention_pa_t_kernel(
                 cols = slice(2 * E * half, 2 * E * (half + 1))
                 nc.sync.dma_start(out=dst[:, cols], in_=view[:, cols])
         for o in (K, Q, V):
+            if o == V:
+                nc.sync.dma_start(out=x_raw[1][:], in_=x_views[1])
             nc.sync.dma_start(
                 out=w_raw[o][:], in_=weights[o].rearrange("(m s) k -> m (s k)", s=SLABS)
             )
@@ -76,7 +76,7 @@ def tile_attention_pa_t_kernel(
                 out=bias_rows[0:1, E * o : E * (o + 1)],
                 in_=biases[o].rearrange("(o n) -> o n", o=1),
             )
-        for g in range(1, GROUPS):
+        for g in range(2, GROUPS):
             nc.sync.dma_start(out=x_raw[g][:], in_=x_views[g])
 
         def weight_mx(name):
@@ -91,6 +91,8 @@ def tile_attention_pa_t_kernel(
         bv_col = consts.tile([P, 2], F32)
         pos_t = consts.tile([P, 4 * E], F32)
 
+        fence = consts.tile([P, 1], U32)
+        k_slabs = {}
         pairs = {}
         x_mx = {}
         xe_mx = {}
@@ -107,9 +109,9 @@ def tile_attention_pa_t_kernel(
                 pairs[n] = work.tile([P, 8 * E], BF16, align_bytes=64, tag="pair", name="pair")
             return pairs[n]
 
-        def turn_words(raw, half, pool, tag):
+        def turn_words(raw, half):
             words = raw[:].bitcast(F32)
-            bank = bank_of(pool, tag)
+            bank = new_bank()
             for s in range(2):
                 start = H * (2 * half + s)
                 for u in range(2):
@@ -119,7 +121,7 @@ def tile_attention_pa_t_kernel(
             return bank
 
         def turn_half(raw, grouped, half, rows_interleaved, copy):
-            bank = turn_words(raw, half, prep_pool, "prep")
+            bank = turn_words(raw, half)
             gwords = grouped.bitcast(F32)
             if rows_interleaved:
                 copy(
@@ -168,8 +170,8 @@ def tile_attention_pa_t_kernel(
         def block(i):
             return slice(P * i, P * (i + 1))
 
-        def stage1_passes(g, j, pool, tag):
-            bank = bank_of(pool, tag)
+        def stage1_passes(g, j):
+            bank = new_bank()
             for t in range(4):
                 mx_pass(bank[:, block(t)], we_mx, block(t), x_mx[g], block(j))
             banks[("s1", j)] = bank
@@ -189,39 +191,45 @@ def tile_attention_pa_t_kernel(
             return staged[(o, j // 2)][:, E * (j % 2) : E * (j % 2 + 1)]
 
         def full_pass(g, j, o):
-            banks[o] = bank_of(s2_pool, "s2")
-            mx_pass(banks[o][:], xe_mx[g], block(j), w_mx[o], slice(0, E))
+            banks[(o, j)] = new_bank()
+            mx_pass(banks[(o, j)][:], xe_mx[g], block(j), w_mx[o], slice(0, E))
+
+        def gpsimd_waits_for_quantise(n):
+            nc.gpsimd.tensor_copy(out=fence[:], in_=xe_mx[n][0][:, 0:1])
 
         def q_exit(j):
             nc.vector.tensor_tensor(
-                out=staged_slab(Q, j), in0=banks[Q][:], in1=bias_all[:, E * Q : E * (Q + 1)], op=ADD
+                out=staged_slab(Q, j), in0=banks[(Q, j)][:], in1=bias_all[:, E * Q : E * (Q + 1)], op=ADD
             )
 
-        def k_exit(j):
-            slab = staged_slab(K, j)
-            nc.scalar.copy(out=slab, in_=banks[K][:])
+        def k_copy(j):
+            k_slabs[j] = staged_slab(K, j)
+            nc.scalar.copy(out=k_slabs[j], in_=banks[(K, j)][:])
+
+        def k_bias(j):
+            slab = k_slabs[j]
             nc.gpsimd.tensor_tensor(
                 out=slab, in0=slab, in1=bias_all[:, E * K : E * (K + 1)], op=ADD
             )
 
-        def v_low_pass(g, j):
-            if j % 2 == 0:
-                banks[V] = bank_of(vlow_pool, "vlow")
-                staged[(V, j // 2)] = stage.tile([P, 2 * E], F32, name="st2", tag="st2")
-            mx_pass(
-                banks[V][:, H * (j % 2) : H * (j % 2 + 1)], xe_mx[g], block(j), w_mx[V], slice(0, H)
-            )
+        def v_low_passes(g, pair):
+            banks[(V, pair)] = new_bank()
+            staged[(V, pair)] = stage.tile([P, 2 * E], F32, name="st2", tag="st2")
+            for j2 in range(2):
+                mx_pass(
+                    banks[(V, pair)][:, H * j2 : H * (j2 + 1)], xe_mx[g], block(2 * pair + j2), w_mx[V], slice(0, H)
+                )
 
         def v_low_exit(pair):
             nc.vector.tensor_tensor(
                 out=staged[(V, pair)][:].rearrange("c (j e) -> c j e", j=2)[:, :, 0:H],
-                in0=banks[V][:].rearrange("c (j e) -> c j e", j=2),
+                in0=banks[(V, pair)][:].rearrange("c (j e) -> c j e", j=2),
                 in1=bias_all[:, E * V : E * V + H].unsqueeze(1).to_broadcast([P, 2, H]),
                 op=ADD,
             )
 
         def v_high_pass(g, i):
-            banks[("vh", i)] = bank_of(s2_pool, "s2")
+            banks[("vh", i)] = new_bank()
             mx_pass(banks[("vh", i)][:], w_mx[V], slice(H + P * i, H + P * (i + 1)), xe_mx[g], slice(0, E))
 
         def v_high_bias(i):
@@ -231,7 +239,7 @@ def tile_attention_pa_t_kernel(
             )
 
         def v_high_back(pair):
-            bank = bank_of(prep_pool, "prep")
+            bank = new_bank()
             for j2 in range(2):
                 for i in range(2):
                     nc.tensor.transpose(
@@ -254,14 +262,14 @@ def tile_attention_pa_t_kernel(
         turn_half(we_raw, grouped_we[:], 0, False, nc.vector.tensor_copy)
         turn_half(we_raw, grouped_we[:], 1, False, nc.scalar.copy)
         turn_x(0)
-        be_bank = bank_of(s2_pool, "s2")
+        be_bank = new_bank()
         for u in range(2):
             nc.tensor.transpose(be_bank[:, block(u)], be_rows[:].bitcast(F32)[:, u:H:2], ident[:])
         nc.scalar.copy(
             out=be_col[:].rearrange("p (u e) -> p u e", u=2),
             in_=be_bank[:].bitcast(BF16).rearrange("p (u w) -> p u w", u=4)[:, 0:2, 0:2],
         )
-        pos_banks = [turn_words(pos_raw, 0, s2_pool, "s2"), turn_words(pos_raw, 1, vlow_pool, "vlow")]
+        pos_banks = [turn_words(pos_raw, 0), turn_words(pos_raw, 1)]
         quantise(grouped_we[:], we_mx)
         quantise_pair(-1)
         grouped_w = {}
@@ -272,17 +280,14 @@ def tile_attention_pa_t_kernel(
                 turn_half(w_raw[o], grouped_w[o][:], half, True, nc.scalar.copy)
 
         def spread_bias(o):
-            bank = bank_of(s2_pool, "s2")
+            bank = new_bank()
             cols = slice(E * o, E * (o + 1))
             nc.tensor.matmul(out=bank[:], lhsT=ones[:], rhs=bias_rows[:, cols], start=True, stop=True)
             nc.scalar.copy(out=bias_all[:, cols], in_=bank[:])
 
         turn_weight(K)
         for j in range(SLABS):
-            if j < 2:
-                stage1_passes(0, j, prep_pool, "prep")
-            else:
-                stage1_passes(0, j, s2_pool, "s2")
+            stage1_passes(0, j)
         for j in range(SLABS):
             nc.vector.tensor_tensor(
                 out=pos_t[:, E * j : E * (j + 1)].rearrange("p (c u e) -> p c u e", u=2, e=2),
@@ -297,15 +302,10 @@ def tile_attention_pa_t_kernel(
         turn_weight(Q)
         turn_x(1)
         turn_weight(V)
-        for o in (V, Q, K):
+        for o in (K, Q, V):
             spread_bias(o)
         quantise(grouped_w[K][:], w_mx[K])
-        quantise(grouped_w[Q][:], w_mx[Q])
-        quantise_pair(0)
-        quantise(grouped_w[V][:], w_mx[V])
-        for j in range(2):
-            stage1_passes(1, j, prep_pool, "prep")
-        bv_bank = bank_of(s2_pool, "s2")
+        bv_bank = new_bank()
         for i in range(2):
             nc.tensor.transpose(
                 bv_bank[:, block(i)], bias_all[:, E * V + H + P * i : E * V + H + P * (i + 1)], ident[:]
@@ -314,54 +314,63 @@ def tile_attention_pa_t_kernel(
             out=bv_col[:].unsqueeze(2),
             in_=bv_bank[:].rearrange("p (i c) -> p i c", c=P)[:, 0:2, 0:1],
         )
-        for j in range(2):
-            stage1_exit(1, j)
 
-        for g in range(GROUPS):
-            for j in range(SLABS):
-                for o in (K, Q) if j == 0 else (Q, K):
-                    full_pass(g, j, o)
-                v_low_pass(g, j)
-                if j == 0:
-                    v_high_pass(g, 0)
-                    v_high_pass(g, 1)
-                if j == 0:
-                    k_exit(j)
-                    q_exit(j)
-                elif j < 3:
-                    q_exit(j)
-                    k_exit(j)
-                else:
-                    k_exit(j)
-                if j == 0:
-                    v_high_bias(0)
-                    v_high_bias(1)
-                    if g + 1 < GROUPS:
-                        stage1_passes(g + 1, 2, prep_pool, "prep")
-                        stage1_passes(g + 1, 3, prep_pool, "prep")
-                        stage1_exit(g + 1, 2)
-                        stage1_exit(g + 1, 3)
-                if j == 1:
-                    v_low_exit(0)
-                    if g + 2 < GROUPS:
-                        turn_x(g + 2)
-                    store(g, Q, 0)
-                if j == 2:
-                    v_high_back(0)
-                    v_high_back(1)
-                if j == 3:
-                    store(g, K, 0)
-                    store(g, V, 0)
-                    if g + 1 < GROUPS:
-                        quantise_pair(g + 1)
-                    if g + 2 < GROUPS:
-                        stage1_passes(g + 2, 0, prep_pool, "prep")
-                        stage1_passes(g + 2, 1, prep_pool, "prep")
-                    q_exit(j)
-                    v_low_exit(1)
-                    if g + 2 < GROUPS:
-                        stage1_exit(g + 2, 0)
-                        stage1_exit(g + 2, 1)
-                    store(g, Q, 1)
-                    store(g, V, 1)
-                    store(g, K, 1)
+        def stage1_unit(g, j):
+            stage1_passes(g, j)
+            stage1_exit(g, j)
+
+        for g in range(GROUPS + 1):
+            if g < GROUPS:
+                quantise_pair(g)
+                gpsimd_waits_for_quantise(g)
+            if g == 0:
+                quantise(grouped_w[Q][:], w_mx[Q])
+                quantise(grouped_w[V][:], w_mx[V])
+            if g + 2 < GROUPS:
+                turn_x(g + 2)
+            if g > 0:
+                q_exit(2)
+                q_exit(3)
+                store(g - 1, Q, 1)
+                v_high_back(0)
+                store(g - 1, V, 0)
+                v_high_back(1)
+                v_low_exit(1)
+                store(g - 1, V, 1)
+                k_bias(2)
+                k_bias(3)
+                store(g - 1, K, 1)
+            if g == GROUPS:
+                break
+            full_pass(g, 0, K)
+            k_copy(0)
+            k_bias(0)
+            if g + 1 < GROUPS:
+                stage1_unit(g + 1, 0)
+            full_pass(g, 1, K)
+            k_copy(1)
+            k_bias(1)
+            store(g, K, 0)
+            if g + 1 < GROUPS:
+                stage1_unit(g + 1, 1)
+            v_high_pass(g, 0)
+            v_high_bias(0)
+            if g + 1 < GROUPS:
+                stage1_unit(g + 1, 2)
+                stage1_unit(g + 1, 3)
+            v_high_pass(g, 1)
+            v_high_bias(1)
+            full_pass(g, 0, Q)
+            q_exit(0)
+            full_pass(g, 1, Q)
+            q_exit(1)
+            store(g, Q, 0)
+            full_pass(g, 2, K)
+            k_copy(2)
+            v_low_passes(g, 0)
+            v_low_exit(0)
+            full_pass(g, 3, K)
+            k_copy(3)
+            full_pass(g, 2, Q)
+            full_pass(g, 3, Q)
+            v_low_passes(g, 1)

@@ -58,24 +58,33 @@ def tile_attention_pa_t_kernel(
         pos_raw = raws.tile([P, 4 * E], BF16)
         pos_view = pos_embed.rearrange("(c j) e -> c (j e)", j=SLABS)
         w_raw = [raws.tile([P, 4 * E], BF16, name="w_raw%d" % o) for o in range(3)]
-        for half in range(2):
-            cols = slice(2 * E * half, 2 * E * (half + 1))
-            nc.sync.dma_start(out=we_raw[:, cols], in_=we_view[:, cols])
-        nc.sync.dma_start(out=be_rows[0:1, :], in_=b_embed.rearrange("(o n) -> o n", o=1))
-        for dst, view in ((x_raw[0], x_views[0]), (pos_raw, pos_view)):
+        def load_halves(dst, view):
             for half in range(2):
                 cols = slice(2 * E * half, 2 * E * (half + 1))
                 nc.sync.dma_start(out=dst[:, cols], in_=view[:, cols])
-        for o in (K, Q, V):
-            if o == V:
-                nc.sync.dma_start(out=x_raw[1][:], in_=x_views[1])
+
+        def load_weight(o):
             nc.sync.dma_start(
                 out=w_raw[o][:], in_=weights[o].rearrange("(m s) k -> m (s k)", s=SLABS)
             )
+
+        def load_bias(o):
             nc.sync.dma_start(
                 out=bias_rows[0:1, E * o : E * (o + 1)],
                 in_=biases[o].rearrange("(o n) -> o n", o=1),
             )
+
+        load_halves(we_raw, we_view)
+        load_halves(x_raw[0], x_views[0])
+        load_halves(pos_raw, pos_view)
+        nc.sync.dma_start(out=be_rows[0:1, :], in_=b_embed.rearrange("(o n) -> o n", o=1))
+        load_bias(K)
+        load_weight(K)
+        load_bias(Q)
+        load_bias(V)
+        load_weight(Q)
+        nc.sync.dma_start(out=x_raw[1][:], in_=x_views[1])
+        load_weight(V)
         for g in range(2, GROUPS):
             nc.sync.dma_start(out=x_raw[g][:], in_=x_views[g])
 
@@ -86,7 +95,7 @@ def tile_attention_pa_t_kernel(
 
         we_mx = weight_mx("we")
         w_mx = [weight_mx("w%d" % o) for o in range(3)]
-        bias_all = consts.tile([P, 3 * E], F32)
+        bias_all = consts.tile([P, 3 * E], BF16)
         be_col = consts.tile([P, 4], F32)
         bv_col = consts.tile([P, 2], F32)
         pos_t = consts.tile([P, 4 * E], F32)
@@ -197,9 +206,9 @@ def tile_attention_pa_t_kernel(
         def gpsimd_waits_for_quantise(n):
             nc.gpsimd.tensor_copy(out=fence[:], in_=xe_mx[n][0][:, 0:1])
 
-        def q_exit(j):
+        def vector_exit(o, j):
             nc.vector.tensor_tensor(
-                out=staged_slab(Q, j), in0=banks[(Q, j)][:], in1=bias_all[:, E * Q : E * (Q + 1)], op=ADD
+                out=staged_slab(o, j), in0=banks[(o, j)][:], in1=bias_all[:, E * o : E * (o + 1)], op=ADD
             )
 
         def k_copy(j):
@@ -262,16 +271,62 @@ def tile_attention_pa_t_kernel(
         turn_half(we_raw, grouped_we[:], 0, False, nc.vector.tensor_copy)
         turn_half(we_raw, grouped_we[:], 1, False, nc.scalar.copy)
         turn_x(0)
+        quantise(grouped_we[:], we_mx)
+        quantise_pair(-1)
         be_bank = new_bank()
         for u in range(2):
             nc.tensor.transpose(be_bank[:, block(u)], be_rows[:].bitcast(F32)[:, u:H:2], ident[:])
+        pos_banks = [turn_words(pos_raw, 0), turn_words(pos_raw, 1)]
         nc.scalar.copy(
             out=be_col[:].rearrange("p (u e) -> p u e", u=2),
             in_=be_bank[:].bitcast(BF16).rearrange("p (u w) -> p u w", u=4)[:, 0:2, 0:2],
         )
-        pos_banks = [turn_words(pos_raw, 0), turn_words(pos_raw, 1)]
-        quantise(grouped_we[:], we_mx)
-        quantise_pair(-1)
+        pos_late = raws.tile([P, 2 * E], BF16)
+        nc.scalar.copy(
+            out=pos_late[:].bitcast(F32).rearrange("p (s m u) -> p s m u", s=2, u=2),
+            in_=pos_banks[1][:].rearrange("p (s u m) -> p s m u", s=2, u=2),
+        )
+        for j in range(2):
+            nc.gpsimd.tensor_tensor(
+                out=pos_t[:, E * (2 + j) : E * (3 + j)].rearrange("p (c t) -> p c t", t=4),
+                in0=pos_late[:, E * j : E * (j + 1)].rearrange("p (c t) -> p c t", t=4),
+                in1=be_col[:].rearrange("p (o t) -> p o t", o=1).to_broadcast([P, P, 4]),
+                op=ADD,
+            )
+        for j in range(2):
+            nc.vector.tensor_tensor(
+                out=pos_t[:, E * j : E * (j + 1)].rearrange("p (c u e) -> p c u e", u=2, e=2),
+                in0=pos_banks[0][:]
+                .bitcast(BF16)
+                .rearrange("p (s u c e) -> p s c u e", s=2, u=2, e=2)[:, j],
+                in1=be_col[:].rearrange("p (o u e) -> p o u e", o=1, u=2).to_broadcast([P, P, 2, 2]),
+                op=ADD,
+            )
+        kq_bank = new_bank()
+        v_bank = new_bank()
+        for bank, o, place in ((kq_bank, Q, 0), (kq_bank, K, 1), (v_bank, V, 0)):
+            nc.tensor.matmul(
+                out=bank[:].bitcast(BF16)[:, E * place : E * (place + 1)],
+                lhsT=ones[:],
+                rhs=bias_rows[:, E * o : E * (o + 1)],
+                start=True,
+                stop=True,
+            )
+        bv_bank = new_bank()
+        for i in range(2):
+            first = E * V + H + P * i
+            nc.tensor.matmul(
+                out=bv_bank[:, 2 * i : 2 * i + 2],
+                lhsT=bias_rows[:, first : first + P],
+                rhs=ones[:, 0:2],
+                start=True,
+                stop=True,
+            )
+        nc.scalar.copy(out=bias_all[:, 0 : 2 * E], in_=kq_bank[:].bitcast(BF16))
+        nc.scalar.copy(out=bias_all[:, 2 * E : 3 * E], in_=v_bank[:].bitcast(BF16)[:, 0:E])
+        nc.scalar.copy(
+            out=bv_col[:].unsqueeze(2), in_=bv_bank[:, 0:4].rearrange("p (i n) -> p i n", n=2)[:, :, 0:1]
+        )
         grouped_w = {}
 
         def turn_weight(o):
@@ -279,66 +334,68 @@ def tile_attention_pa_t_kernel(
             for half in range(2):
                 turn_half(w_raw[o], grouped_w[o][:], half, True, nc.scalar.copy)
 
-        def spread_bias(o):
-            bank = new_bank()
-            cols = slice(E * o, E * (o + 1))
-            nc.tensor.matmul(out=bank[:], lhsT=ones[:], rhs=bias_rows[:, cols], start=True, stop=True)
-            nc.scalar.copy(out=bias_all[:, cols], in_=bank[:])
-
         turn_weight(K)
         for j in range(SLABS):
             stage1_passes(0, j)
         for j in range(SLABS):
-            nc.vector.tensor_tensor(
-                out=pos_t[:, E * j : E * (j + 1)].rearrange("p (c u e) -> p c u e", u=2, e=2),
-                in0=pos_banks[j // 2][:]
-                .bitcast(BF16)
-                .rearrange("p (s u c e) -> p s c u e", s=2, u=2, e=2)[:, j % 2],
-                in1=be_col[:].rearrange("p (o u e) -> p o u e", o=1, u=2).to_broadcast([P, P, 2, 2]),
-                op=ADD,
-            )
-        for j in range(SLABS):
             stage1_exit(0, j)
+        quantise(grouped_w[K][:], w_mx[K])
         turn_weight(Q)
         turn_x(1)
         turn_weight(V)
-        for o in (K, Q, V):
-            spread_bias(o)
-        quantise(grouped_w[K][:], w_mx[K])
-        bv_bank = new_bank()
-        for i in range(2):
-            nc.tensor.transpose(
-                bv_bank[:, block(i)], bias_all[:, E * V + H + P * i : E * V + H + P * (i + 1)], ident[:]
-            )
-        nc.scalar.copy(
-            out=bv_col[:].unsqueeze(2),
-            in_=bv_bank[:].rearrange("p (i c) -> p i c", c=P)[:, 0:2, 0:1],
-        )
 
         def stage1_unit(g, j):
             stage1_passes(g, j)
             stage1_exit(g, j)
 
-        for g in range(GROUPS + 1):
+        first_codes = work.tile([P, 2 * E], U32, align_bytes=64, tag="codes", name="codes")
+        first_scales = work.tile([P, 2 * E], U8, align_bytes=64, tag="scales", name="scales")
+        xe_mx[0] = (first_codes[:, 0:E], first_scales[:, 0:E])
+        x_mx[1] = (first_codes[:, E : 2 * E], first_scales[:, E : 2 * E])
+        quantise(pair_of(0)[:, 0 : 4 * E], xe_mx[0])
+        quantise(grouped_w[Q][:], w_mx[Q])
+        quantise(pair_of(0)[:, 4 * E : 8 * E], x_mx[1])
+        quantise(grouped_w[V][:], w_mx[V])
+        nc.gpsimd.tensor_copy(out=fence[:], in_=w_mx[V][0][:, 0:1])
+        for j in range(SLABS):
+            full_pass(0, j, K)
+            if j < 3:
+                k_copy(j)
+                k_bias(j)
+            full_pass(0, j, Q)
+            vector_exit(Q, j)
+            if j == 3:
+                vector_exit(K, j)
+            if j % 2 == 1:
+                store(0, Q, j // 2)
+                store(0, K, j // 2)
+        for j in range(SLABS):
+            stage1_unit(1, j)
+        for i in range(2):
+            v_high_pass(0, i)
+            v_high_bias(i)
+        v_low_passes(0, 0)
+        v_low_exit(0)
+        turn_x(2)
+        v_low_passes(0, 1)
+
+        for g in range(1, GROUPS + 1):
             if g < GROUPS:
                 quantise_pair(g)
                 gpsimd_waits_for_quantise(g)
-            if g == 0:
-                quantise(grouped_w[Q][:], w_mx[Q])
-                quantise(grouped_w[V][:], w_mx[V])
             if g + 2 < GROUPS:
                 turn_x(g + 2)
-            if g > 0:
-                q_exit(2)
-                q_exit(3)
+            if g > 1:
+                vector_exit(Q, 3)
                 store(g - 1, Q, 1)
-                v_high_back(0)
-                store(g - 1, V, 0)
-                v_high_back(1)
-                v_low_exit(1)
-                store(g - 1, V, 1)
+                vector_exit(K, 3)
+            v_high_back(0)
+            store(g - 1, V, 0)
+            v_high_back(1)
+            v_low_exit(1)
+            store(g - 1, V, 1)
+            if g > 1:
                 k_bias(2)
-                k_bias(3)
                 store(g - 1, K, 1)
             if g == GROUPS:
                 break
@@ -361,16 +418,16 @@ def tile_attention_pa_t_kernel(
             v_high_pass(g, 1)
             v_high_bias(1)
             full_pass(g, 0, Q)
-            q_exit(0)
+            vector_exit(Q, 0)
             full_pass(g, 1, Q)
-            q_exit(1)
+            vector_exit(Q, 1)
             store(g, Q, 0)
             full_pass(g, 2, K)
             k_copy(2)
             v_low_passes(g, 0)
             v_low_exit(0)
-            full_pass(g, 3, K)
-            k_copy(3)
             full_pass(g, 2, Q)
+            vector_exit(Q, 2)
             full_pass(g, 3, Q)
+            full_pass(g, 3, K)
             v_low_passes(g, 1)

@@ -33,7 +33,7 @@ def tile_attention_pa_t_kernel(
         consts = ctx.enter_context(tc.tile_pool(name="consts", bufs=1))
         raws = ctx.enter_context(tc.tile_pool(name="raws", bufs=1))
         work = ctx.enter_context(tc.tile_pool(name="work", bufs=2))
-        stage = ctx.enter_context(tc.tile_pool(name="stage", bufs=4))
+        stage = ctx.enter_context(tc.tile_pool(name="stage", bufs=7))
         bank_pool = ctx.enter_context(tc.psum_pool(name="banks", bufs=8))
         ctx.enter_context(tc.manual_schedule())
 
@@ -75,16 +75,15 @@ def tile_attention_pa_t_kernel(
             )
 
         load_halves(we_raw, we_view)
-        load_halves(x_raw[0], x_views[0])
-        load_halves(pos_raw, pos_view)
         nc.sync.dma_start(out=be_rows[0:1, :], in_=b_embed.rearrange("(o n) -> o n", o=1))
-        load_bias(K)
-        load_weight(K)
-        load_bias(Q)
-        load_bias(V)
+        load_halves(pos_raw, pos_view)
+        load_halves(x_raw[0], x_views[0])
+        for o in (Q, K, V):
+            load_bias(o)
         load_weight(Q)
-        nc.sync.dma_start(out=x_raw[1][:], in_=x_views[1])
+        load_weight(K)
         load_weight(V)
+        nc.sync.dma_start(out=x_raw[1][:], in_=x_views[1])
         for g in range(2, GROUPS):
             nc.sync.dma_start(out=x_raw[g][:], in_=x_views[g])
 
@@ -194,6 +193,11 @@ def tile_attention_pa_t_kernel(
                 op=ADD,
             )
 
+        def staged_pair(g, o, pair):
+            if (g, o, pair) not in staged:
+                staged[(g, o, pair)] = stage.tile([P, 2 * E], F32, name="st%d" % o, tag="st%d" % o)
+            return staged[(g, o, pair)]
+
         def staged_slab(o, j):
             if j % 2 == 0:
                 staged[(o, j // 2)] = stage.tile([P, 2 * E], F32, name="st%d" % o, tag="st%d" % o)
@@ -221,17 +225,25 @@ def tile_attention_pa_t_kernel(
                 out=slab, in0=slab, in1=bias_all[:, E * K : E * (K + 1)], op=ADD
             )
 
+        def k_bias_pair(pair):
+            both = staged[(K, pair)][:].rearrange("c (j e) -> c j e", j=2)
+            nc.gpsimd.tensor_tensor(
+                out=both,
+                in0=both,
+                in1=bias_all[:, E * K : E * (K + 1)].unsqueeze(1).to_broadcast([P, 2, E]),
+                op=ADD,
+            )
+
         def v_low_passes(g, pair):
             banks[(V, pair)] = new_bank()
-            staged[(V, pair)] = stage.tile([P, 2 * E], F32, name="st2", tag="st2")
             for j2 in range(2):
                 mx_pass(
                     banks[(V, pair)][:, H * j2 : H * (j2 + 1)], xe_mx[g], block(2 * pair + j2), w_mx[V], slice(0, H)
                 )
 
-        def v_low_exit(pair):
+        def v_low_exit(g, pair):
             nc.vector.tensor_tensor(
-                out=staged[(V, pair)][:].rearrange("c (j e) -> c j e", j=2)[:, :, 0:H],
+                out=staged_pair(g, V, pair)[:].rearrange("c (j e) -> c j e", j=2)[:, :, 0:H],
                 in0=banks[(V, pair)][:].rearrange("c (j e) -> c j e", j=2),
                 in1=bias_all[:, E * V : E * V + H].unsqueeze(1).to_broadcast([P, 2, H]),
                 op=ADD,
@@ -247,7 +259,7 @@ def tile_attention_pa_t_kernel(
                 out=v_high[i][:], in_=banks[("vh", i)][:], func=IDENTITY, bias=bv_col[:, i : i + 1]
             )
 
-        def v_high_back(pair):
+        def v_high_back(g, pair):
             bank = new_bank()
             for j2 in range(2):
                 for i in range(2):
@@ -255,7 +267,7 @@ def tile_attention_pa_t_kernel(
                         bank[:, block(2 * j2 + i)], v_high[i][:, block(2 * pair + j2)], ident[:]
                     )
             nc.scalar.copy(
-                out=staged[(V, pair)][:].rearrange("c (j e) -> c j e", j=2)[:, :, H:E],
+                out=staged_pair(g, V, pair)[:].rearrange("c (j e) -> c j e", j=2)[:, :, H:E],
                 in_=bank[:].rearrange("c (j e) -> c j e", j=2),
             )
 
@@ -264,44 +276,46 @@ def tile_attention_pa_t_kernel(
                 out=outs[o][g].rearrange("(c j) h d -> c (j h d)", j=SLABS)[
                     :, 2 * E * pair : 2 * E * (pair + 1)
                 ],
-                in_=staged[(o, pair)][:],
+                in_=(staged_pair(g, V, pair) if o == V else staged[(o, pair)])[:],
             )
 
         grouped_we = new_grouped()
         turn_half(we_raw, grouped_we[:], 0, False, nc.vector.tensor_copy)
         turn_half(we_raw, grouped_we[:], 1, False, nc.scalar.copy)
-        turn_x(0)
-        quantise(grouped_we[:], we_mx)
-        quantise_pair(-1)
         be_bank = new_bank()
         for u in range(2):
             nc.tensor.transpose(be_bank[:, block(u)], be_rows[:].bitcast(F32)[:, u:H:2], ident[:])
-        pos_banks = [turn_words(pos_raw, 0), turn_words(pos_raw, 1)]
         nc.scalar.copy(
             out=be_col[:].rearrange("p (u e) -> p u e", u=2),
             in_=be_bank[:].bitcast(BF16).rearrange("p (u w) -> p u w", u=4)[:, 0:2, 0:2],
         )
-        pos_late = raws.tile([P, 2 * E], BF16)
-        nc.scalar.copy(
-            out=pos_late[:].bitcast(F32).rearrange("p (s m u) -> p s m u", s=2, u=2),
-            in_=pos_banks[1][:].rearrange("p (s u m) -> p s m u", s=2, u=2),
-        )
-        for j in range(2):
-            nc.gpsimd.tensor_tensor(
-                out=pos_t[:, E * (2 + j) : E * (3 + j)].rearrange("p (c t) -> p c t", t=4),
-                in0=pos_late[:, E * j : E * (j + 1)].rearrange("p (c t) -> p c t", t=4),
-                in1=be_col[:].rearrange("p (o t) -> p o t", o=1).to_broadcast([P, P, 4]),
-                op=ADD,
-            )
-        for j in range(2):
+        pos_banks = [turn_words(pos_raw, 0), turn_words(pos_raw, 1)]
+        quantise(grouped_we[:], we_mx)
+        for j in range(SLABS):
             nc.vector.tensor_tensor(
                 out=pos_t[:, E * j : E * (j + 1)].rearrange("p (c u e) -> p c u e", u=2, e=2),
-                in0=pos_banks[0][:]
+                in0=pos_banks[j // 2][:]
                 .bitcast(BF16)
-                .rearrange("p (s u c e) -> p s c u e", s=2, u=2, e=2)[:, j],
+                .rearrange("p (s u c e) -> p s c u e", s=2, u=2, e=2)[:, j % 2],
                 in1=be_col[:].rearrange("p (o u e) -> p o u e", o=1, u=2).to_broadcast([P, P, 2, 2]),
                 op=ADD,
             )
+        turn_x(0)
+        quantise_pair(-1)
+        grouped_w = {}
+
+        def turn_weight(o):
+            grouped_w[o] = new_grouped()
+            for half in range(2):
+                turn_half(w_raw[o], grouped_w[o][:], half, True, nc.scalar.copy)
+
+        turn_weight(Q)
+        turn_weight(K)
+        for j in range(SLABS):
+            stage1_passes(0, j)
+        quantise(grouped_w[Q][:], w_mx[Q])
+        for j in range(SLABS):
+            stage1_exit(0, j)
         kq_bank = new_bank()
         v_bank = new_bank()
         for bank, o, place in ((kq_bank, Q, 0), (kq_bank, K, 1), (v_bank, V, 0)):
@@ -327,21 +341,6 @@ def tile_attention_pa_t_kernel(
         nc.scalar.copy(
             out=bv_col[:].unsqueeze(2), in_=bv_bank[:, 0:4].rearrange("p (i n) -> p i n", n=2)[:, :, 0:1]
         )
-        grouped_w = {}
-
-        def turn_weight(o):
-            grouped_w[o] = new_grouped()
-            for half in range(2):
-                turn_half(w_raw[o], grouped_w[o][:], half, True, nc.scalar.copy)
-
-        turn_weight(K)
-        for j in range(SLABS):
-            stage1_passes(0, j)
-        for j in range(SLABS):
-            stage1_exit(0, j)
-        quantise(grouped_w[K][:], w_mx[K])
-        turn_weight(Q)
-        turn_x(1)
         turn_weight(V)
 
         def stage1_unit(g, j):
@@ -353,81 +352,96 @@ def tile_attention_pa_t_kernel(
         xe_mx[0] = (first_codes[:, 0:E], first_scales[:, 0:E])
         x_mx[1] = (first_codes[:, E : 2 * E], first_scales[:, E : 2 * E])
         quantise(pair_of(0)[:, 0 : 4 * E], xe_mx[0])
-        quantise(grouped_w[Q][:], w_mx[Q])
-        quantise(pair_of(0)[:, 4 * E : 8 * E], x_mx[1])
-        quantise(grouped_w[V][:], w_mx[V])
-        nc.gpsimd.tensor_copy(out=fence[:], in_=w_mx[V][0][:, 0:1])
+        quantise(grouped_w[K][:], w_mx[K])
         for j in range(SLABS):
-            full_pass(0, j, K)
-            if j < 3:
-                k_copy(j)
-                k_bias(j)
             full_pass(0, j, Q)
             vector_exit(Q, j)
-            if j == 3:
-                vector_exit(K, j)
             if j % 2 == 1:
                 store(0, Q, j // 2)
-                store(0, K, j // 2)
+        turn_x(1)
+        quantise(grouped_w[V][:], w_mx[V])
         for j in range(SLABS):
-            stage1_unit(1, j)
+            full_pass(0, j, K)
+            if j < 2:
+                vector_exit(K, j)
+                if j == 1:
+                    store(0, K, 0)
+            else:
+                k_copy(j)
+        quantise(pair_of(0)[:, 4 * E : 8 * E], x_mx[1])
+        nc.gpsimd.tensor_copy(out=fence[:], in_=x_mx[1][0][:, 0:1])
+        k_bias_pair(1)
+        store(0, K, 1)
         for i in range(2):
             v_high_pass(0, i)
             v_high_bias(i)
         v_low_passes(0, 0)
-        v_low_exit(0)
+        v_low_exit(0, 0)
+        for j in range(2):
+            stage1_unit(1, j)
+        for j in range(2, SLABS):
+            stage1_unit(1, j)
         turn_x(2)
+        for pair in range(2):
+            v_high_back(0, pair)
+        store(0, V, 0)
         v_low_passes(0, 1)
 
         for g in range(1, GROUPS + 1):
             if g < GROUPS:
                 quantise_pair(g)
                 gpsimd_waits_for_quantise(g)
+            if g > 1:
+                v_high_back(g - 1, 0)
+                v_high_back(g - 1, 1)
             if g + 2 < GROUPS:
                 turn_x(g + 2)
             if g > 1:
+                vector_exit(Q, 2)
                 vector_exit(Q, 3)
                 store(g - 1, Q, 1)
-                vector_exit(K, 3)
-            v_high_back(0)
-            store(g - 1, V, 0)
-            v_high_back(1)
-            v_low_exit(1)
+                store(g - 1, V, 0)
+            v_low_exit(g - 1, 1)
             store(g - 1, V, 1)
-            if g > 1:
-                k_bias(2)
+            if g > 1 and g < GROUPS:
+                k_bias_pair(1)
                 store(g - 1, K, 1)
             if g == GROUPS:
                 break
-            full_pass(g, 0, K)
-            k_copy(0)
-            k_bias(0)
-            if g + 1 < GROUPS:
-                stage1_unit(g + 1, 0)
-            full_pass(g, 1, K)
-            k_copy(1)
-            k_bias(1)
-            store(g, K, 0)
-            if g + 1 < GROUPS:
-                stage1_unit(g + 1, 1)
-            v_high_pass(g, 0)
-            v_high_bias(0)
-            if g + 1 < GROUPS:
-                stage1_unit(g + 1, 2)
-                stage1_unit(g + 1, 3)
-            v_high_pass(g, 1)
-            v_high_bias(1)
+
+            def next_stage1(j):
+                if g + 1 < GROUPS:
+                    stage1_unit(g + 1, j)
+
+            for j in range(2):
+                full_pass(g, j, K)
+                k_copy(j)
+            k_bias_pair(0)
             full_pass(g, 0, Q)
             vector_exit(Q, 0)
+            next_stage1(0)
             full_pass(g, 1, Q)
             vector_exit(Q, 1)
             store(g, Q, 0)
-            full_pass(g, 2, K)
-            k_copy(2)
+            store(g, K, 0)
+            next_stage1(1)
+            if g == GROUPS - 1:
+                for j in (2, 3):
+                    full_pass(g, j, K)
+                    vector_exit(K, j)
+                store(g, K, 1)
+            v_high_pass(g, 0)
+            v_high_bias(0)
+            next_stage1(2)
+            v_high_pass(g, 1)
+            v_high_bias(1)
+            next_stage1(3)
             v_low_passes(g, 0)
-            v_low_exit(0)
-            full_pass(g, 2, Q)
-            vector_exit(Q, 2)
-            full_pass(g, 3, Q)
-            full_pass(g, 3, K)
+            v_low_exit(g, 0)
+            if g < GROUPS - 1:
+                for j in (2, 3):
+                    full_pass(g, j, K)
+                    k_copy(j)
+            for j in (2, 3):
+                full_pass(g, j, Q)
             v_low_passes(g, 1)

@@ -34,11 +34,15 @@ def tile_attention_pa_t_kernel(
         raws = ctx.enter_context(tc.tile_pool(name="raws", bufs=1))
         work = ctx.enter_context(tc.tile_pool(name="work", bufs=2))
         stage = ctx.enter_context(tc.tile_pool(name="stage", bufs=7))
-        bank_pool = ctx.enter_context(tc.psum_pool(name="banks", bufs=8))
+        vector_banks = ctx.enter_context(tc.psum_pool(name="vector_banks", bufs=4))
+        scalar_banks = ctx.enter_context(tc.psum_pool(name="scalar_banks", bufs=4))
         ctx.enter_context(tc.manual_schedule())
 
-        def new_bank():
-            return bank_pool.tile([P, E], F32, tag="bank", name="bank")
+        def vector_bank():
+            return vector_banks.tile([P, E], F32, tag="vbank", name="vbank")
+
+        def scalar_bank():
+            return scalar_banks.tile([P, E], F32, tag="sbank", name="sbank")
 
         ident = consts.tile([P, P], F32)
         make_identity(nc, ident[:])
@@ -58,6 +62,7 @@ def tile_attention_pa_t_kernel(
         pos_raw = raws.tile([P, 4 * E], BF16)
         pos_view = pos_embed.rearrange("(c j) e -> c (j e)", j=SLABS)
         w_raw = [raws.tile([P, 4 * E], BF16, name="w_raw%d" % o) for o in range(3)]
+
         def load_halves(dst, view):
             for half in range(2):
                 cols = slice(2 * E * half, 2 * E * (half + 1))
@@ -75,13 +80,13 @@ def tile_attention_pa_t_kernel(
             )
 
         load_halves(we_raw, we_view)
-        nc.sync.dma_start(out=be_rows[0:1, :], in_=b_embed.rearrange("(o n) -> o n", o=1))
         load_halves(pos_raw, pos_view)
+        nc.sync.dma_start(out=be_rows[0:1, :], in_=b_embed.rearrange("(o n) -> o n", o=1))
         load_halves(x_raw[0], x_views[0])
+        load_halves(w_raw[Q], weights[Q].rearrange("(m s) k -> m (s k)", s=SLABS))
+        load_weight(K)
         for o in (Q, K, V):
             load_bias(o)
-        load_weight(Q)
-        load_weight(K)
         load_weight(V)
         nc.sync.dma_start(out=x_raw[1][:], in_=x_views[1])
         for g in range(2, GROUPS):
@@ -101,6 +106,7 @@ def tile_attention_pa_t_kernel(
 
         fence = consts.tile([P, 1], U32)
         k_slabs = {}
+        x_even_odd = {}
         pairs = {}
         x_mx = {}
         xe_mx = {}
@@ -117,19 +123,30 @@ def tile_attention_pa_t_kernel(
                 pairs[n] = work.tile([P, 8 * E], BF16, align_bytes=64, tag="pair", name="pair")
             return pairs[n]
 
-        def turn_words(raw, half):
+        def spread_words(g, half):
+            if half == 0:
+                x_even_odd[g] = work.tile([P, 4 * E], BF16, tag="x_even_odd", name="x_even_odd", bufs=2)
+            cols = slice(2 * E * half, 2 * E * (half + 1))
+            nc.scalar.copy(
+                out=x_even_odd[g][:, cols].bitcast(F32).rearrange("p (s u m) -> p s u m", s=2, u=2),
+                in_=x_raw[g][:, cols].bitcast(F32).rearrange("p (s m u) -> p s u m", s=2, u=2),
+            )
+
+        def turn_words(raw, half, new_bank, apart=False):
             words = raw[:].bitcast(F32)
             bank = new_bank()
             for s in range(2):
                 start = H * (2 * half + s)
                 for u in range(2):
-                    nc.tensor.transpose(
-                        bank[:, block(2 * s + u)], words[:, start + u : start + H : 2], ident[:]
-                    )
+                    if apart:
+                        cols = slice(start + P * u, start + P * (u + 1))
+                    else:
+                        cols = slice(start + u, start + H, 2)
+                    nc.tensor.transpose(bank[:, block(2 * s + u)], words[:, cols], ident[:])
             return bank
 
-        def turn_half(raw, grouped, half, rows_interleaved, copy):
-            bank = turn_words(raw, half)
+        def turn_half(raw, grouped, half, rows_interleaved, copy, apart=False, on_vec=False):
+            bank = turn_words(raw, half, vector_bank if on_vec else scalar_bank, apart)
             gwords = grouped.bitcast(F32)
             if rows_interleaved:
                 copy(
@@ -148,7 +165,9 @@ def tile_attention_pa_t_kernel(
 
         def turn_x(g):
             for half in range(2):
-                turn_half(x_raw[g], pair_of(g - 1)[:, 4 * E : 8 * E], half, False, nc.scalar.copy)
+                apart = g in x_even_odd
+                raw = x_even_odd[g] if apart else x_raw[g]
+                turn_half(raw, pair_of(g - 1)[:, 4 * E : 8 * E], half, False, nc.scalar.copy, apart)
 
         def quantise(grouped, mx):
             nc.vector.quantize_mx(out=mx[0].bitcast(FP8X4), scales=mx[1], in_=grouped)
@@ -179,7 +198,7 @@ def tile_attention_pa_t_kernel(
             return slice(P * i, P * (i + 1))
 
         def stage1_passes(g, j):
-            bank = new_bank()
+            bank = vector_bank()
             for t in range(4):
                 mx_pass(bank[:, block(t)], we_mx, block(t), x_mx[g], block(j))
             banks[("s1", j)] = bank
@@ -203,7 +222,7 @@ def tile_attention_pa_t_kernel(
                 staged[(o, j // 2)] = stage.tile([P, 2 * E], F32, name="st%d" % o, tag="st%d" % o)
             return staged[(o, j // 2)][:, E * (j % 2) : E * (j % 2 + 1)]
 
-        def full_pass(g, j, o):
+        def full_pass(g, j, o, new_bank):
             banks[(o, j)] = new_bank()
             mx_pass(banks[(o, j)][:], xe_mx[g], block(j), w_mx[o], slice(0, E))
 
@@ -219,12 +238,6 @@ def tile_attention_pa_t_kernel(
             k_slabs[j] = staged_slab(K, j)
             nc.scalar.copy(out=k_slabs[j], in_=banks[(K, j)][:])
 
-        def k_bias(j):
-            slab = k_slabs[j]
-            nc.gpsimd.tensor_tensor(
-                out=slab, in0=slab, in1=bias_all[:, E * K : E * (K + 1)], op=ADD
-            )
-
         def k_bias_pair(pair):
             both = staged[(K, pair)][:].rearrange("c (j e) -> c j e", j=2)
             nc.gpsimd.tensor_tensor(
@@ -235,7 +248,7 @@ def tile_attention_pa_t_kernel(
             )
 
         def v_low_passes(g, pair):
-            banks[(V, pair)] = new_bank()
+            banks[(V, pair)] = vector_bank()
             for j2 in range(2):
                 mx_pass(
                     banks[(V, pair)][:, H * j2 : H * (j2 + 1)], xe_mx[g], block(2 * pair + j2), w_mx[V], slice(0, H)
@@ -250,7 +263,7 @@ def tile_attention_pa_t_kernel(
             )
 
         def v_high_pass(g, i):
-            banks[("vh", i)] = new_bank()
+            banks[("vh", i)] = scalar_bank()
             mx_pass(banks[("vh", i)][:], w_mx[V], slice(H + P * i, H + P * (i + 1)), xe_mx[g], slice(0, E))
 
         def v_high_bias(i):
@@ -260,7 +273,7 @@ def tile_attention_pa_t_kernel(
             )
 
         def v_high_back(g, pair):
-            bank = new_bank()
+            bank = scalar_bank()
             for j2 in range(2):
                 for i in range(2):
                     nc.tensor.transpose(
@@ -280,16 +293,16 @@ def tile_attention_pa_t_kernel(
             )
 
         grouped_we = new_grouped()
-        turn_half(we_raw, grouped_we[:], 0, False, nc.vector.tensor_copy)
+        turn_half(we_raw, grouped_we[:], 0, False, nc.vector.tensor_copy, on_vec=True)
         turn_half(we_raw, grouped_we[:], 1, False, nc.scalar.copy)
-        be_bank = new_bank()
+        pos_banks = [turn_words(pos_raw, 0, vector_bank), turn_words(pos_raw, 1, vector_bank)]
+        be_bank = scalar_bank()
         for u in range(2):
             nc.tensor.transpose(be_bank[:, block(u)], be_rows[:].bitcast(F32)[:, u:H:2], ident[:])
         nc.scalar.copy(
             out=be_col[:].rearrange("p (u e) -> p u e", u=2),
             in_=be_bank[:].bitcast(BF16).rearrange("p (u w) -> p u w", u=4)[:, 0:2, 0:2],
         )
-        pos_banks = [turn_words(pos_raw, 0), turn_words(pos_raw, 1)]
         quantise(grouped_we[:], we_mx)
         for j in range(SLABS):
             nc.vector.tensor_tensor(
@@ -316,8 +329,9 @@ def tile_attention_pa_t_kernel(
         quantise(grouped_w[Q][:], w_mx[Q])
         for j in range(SLABS):
             stage1_exit(0, j)
-        kq_bank = new_bank()
-        v_bank = new_bank()
+        turn_weight(V)
+        kq_bank = scalar_bank()
+        v_bank = scalar_bank()
         for bank, o, place in ((kq_bank, Q, 0), (kq_bank, K, 1), (v_bank, V, 0)):
             nc.tensor.matmul(
                 out=bank[:].bitcast(BF16)[:, E * place : E * (place + 1)],
@@ -326,7 +340,7 @@ def tile_attention_pa_t_kernel(
                 start=True,
                 stop=True,
             )
-        bv_bank = new_bank()
+        bv_bank = scalar_bank()
         for i in range(2):
             first = E * V + H + P * i
             nc.tensor.matmul(
@@ -341,7 +355,6 @@ def tile_attention_pa_t_kernel(
         nc.scalar.copy(
             out=bv_col[:].unsqueeze(2), in_=bv_bank[:, 0:4].rearrange("p (i n) -> p i n", n=2)[:, :, 0:1]
         )
-        turn_weight(V)
 
         def stage1_unit(g, j):
             stage1_passes(g, j)
@@ -353,23 +366,23 @@ def tile_attention_pa_t_kernel(
         x_mx[1] = (first_codes[:, E : 2 * E], first_scales[:, E : 2 * E])
         quantise(pair_of(0)[:, 0 : 4 * E], xe_mx[0])
         quantise(grouped_w[K][:], w_mx[K])
+        quantise(grouped_w[V][:], w_mx[V])
         for j in range(SLABS):
-            full_pass(0, j, Q)
+            full_pass(0, j, Q, vector_bank)
             vector_exit(Q, j)
             if j % 2 == 1:
                 store(0, Q, j // 2)
         turn_x(1)
-        quantise(grouped_w[V][:], w_mx[V])
+        quantise(pair_of(0)[:, 4 * E : 8 * E], x_mx[1])
+        nc.gpsimd.tensor_copy(out=fence[:], in_=x_mx[1][0][:, 0:1])
         for j in range(SLABS):
-            full_pass(0, j, K)
+            full_pass(0, j, K, vector_bank if j < 2 else scalar_bank)
             if j < 2:
                 vector_exit(K, j)
                 if j == 1:
                     store(0, K, 0)
             else:
                 k_copy(j)
-        quantise(pair_of(0)[:, 4 * E : 8 * E], x_mx[1])
-        nc.gpsimd.tensor_copy(out=fence[:], in_=x_mx[1][0][:, 0:1])
         k_bias_pair(1)
         store(0, K, 1)
         for i in range(2):
@@ -379,9 +392,9 @@ def tile_attention_pa_t_kernel(
         v_low_exit(0, 0)
         for j in range(2):
             stage1_unit(1, j)
+        turn_x(2)
         for j in range(2, SLABS):
             stage1_unit(1, j)
-        turn_x(2)
         for pair in range(2):
             v_high_back(0, pair)
         store(0, V, 0)
@@ -413,35 +426,39 @@ def tile_attention_pa_t_kernel(
                 if g + 1 < GROUPS:
                     stage1_unit(g + 1, j)
 
+            full_pass(g, 0, Q, vector_bank)
+            vector_exit(Q, 0)
             for j in range(2):
-                full_pass(g, j, K)
+                full_pass(g, j, K, vector_bank if g == GROUPS - 1 and j > 1 else scalar_bank)
                 k_copy(j)
             k_bias_pair(0)
-            full_pass(g, 0, Q)
-            vector_exit(Q, 0)
             next_stage1(0)
-            full_pass(g, 1, Q)
+            full_pass(g, 1, Q, vector_bank)
             vector_exit(Q, 1)
             store(g, Q, 0)
             store(g, K, 0)
             next_stage1(1)
             if g == GROUPS - 1:
                 for j in (2, 3):
-                    full_pass(g, j, K)
+                    full_pass(g, j, K, vector_bank if g == GROUPS - 1 and j > 1 else scalar_bank)
                     vector_exit(K, j)
                 store(g, K, 1)
+            if g + 3 < GROUPS:
+                spread_words(g + 3, 0)
             v_high_pass(g, 0)
             v_high_bias(0)
             next_stage1(2)
             v_high_pass(g, 1)
             v_high_bias(1)
+            if g + 3 < GROUPS:
+                spread_words(g + 3, 1)
             next_stage1(3)
             v_low_passes(g, 0)
             v_low_exit(g, 0)
             if g < GROUPS - 1:
                 for j in (2, 3):
-                    full_pass(g, j, K)
+                    full_pass(g, j, K, vector_bank if g == GROUPS - 1 and j > 1 else scalar_bank)
                     k_copy(j)
             for j in (2, 3):
-                full_pass(g, j, Q)
+                full_pass(g, j, Q, vector_bank)
             v_low_passes(g, 1)

@@ -74,19 +74,19 @@ def tile_attention_pa_t_kernel(
             )
 
         def load_bias(o):
-            nc.sync.dma_start(
+            nc.scalar.dma_start(
                 out=bias_rows[0:1, E * o : E * (o + 1)],
                 in_=biases[o].rearrange("(o n) -> o n", o=1),
             )
 
         load_halves(we_raw, we_view)
+        nc.scalar.dma_start(out=be_rows[0:1, :], in_=b_embed.rearrange("(o n) -> o n", o=1))
+        for o in (Q, K, V):
+            load_bias(o)
         load_halves(pos_raw, pos_view)
-        nc.sync.dma_start(out=be_rows[0:1, :], in_=b_embed.rearrange("(o n) -> o n", o=1))
         load_halves(x_raw[0], x_views[0])
         load_halves(w_raw[Q], weights[Q].rearrange("(m s) k -> m (s k)", s=SLABS))
         load_weight(K)
-        for o in (Q, K, V):
-            load_bias(o)
         load_weight(V)
         nc.sync.dma_start(out=x_raw[1][:], in_=x_views[1])
         for g in range(2, GROUPS):
@@ -212,10 +212,10 @@ def tile_attention_pa_t_kernel(
                 op=ADD,
             )
 
-        def staged_pair(g, o, pair):
-            if (g, o, pair) not in staged:
-                staged[(g, o, pair)] = stage.tile([P, 2 * E], F32, name="st%d" % o, tag="st%d" % o)
-            return staged[(g, o, pair)]
+        def staged_v(g, pair):
+            if (g, V) not in staged:
+                staged[(g, V)] = stage.tile([P, 4 * E], F32, name="st_v", tag="st_v", bufs=4)
+            return staged[(g, V)][:, 2 * E * pair : 2 * E * (pair + 1)]
 
         def staged_slab(o, j):
             if j % 2 == 0:
@@ -256,7 +256,7 @@ def tile_attention_pa_t_kernel(
 
         def v_low_exit(g, pair):
             nc.vector.tensor_tensor(
-                out=staged_pair(g, V, pair)[:].rearrange("c (j e) -> c j e", j=2)[:, :, 0:H],
+                out=staged_v(g, pair).rearrange("c (j e) -> c j e", j=2)[:, :, 0:H],
                 in0=banks[(V, pair)][:].rearrange("c (j e) -> c j e", j=2),
                 in1=bias_all[:, E * V : E * V + H].unsqueeze(1).to_broadcast([P, 2, H]),
                 op=ADD,
@@ -280,7 +280,7 @@ def tile_attention_pa_t_kernel(
                         bank[:, block(2 * j2 + i)], v_high[i][:, block(2 * pair + j2)], ident[:]
                     )
             nc.scalar.copy(
-                out=staged_pair(g, V, pair)[:].rearrange("c (j e) -> c j e", j=2)[:, :, H:E],
+                out=staged_v(g, pair).rearrange("c (j e) -> c j e", j=2)[:, :, H:E],
                 in_=bank[:].rearrange("c (j e) -> c j e", j=2),
             )
 
@@ -289,7 +289,12 @@ def tile_attention_pa_t_kernel(
                 out=outs[o][g].rearrange("(c j) h d -> c (j h d)", j=SLABS)[
                     :, 2 * E * pair : 2 * E * (pair + 1)
                 ],
-                in_=(staged_pair(g, V, pair) if o == V else staged[(o, pair)])[:],
+                in_=staged_v(g, pair) if o == V else staged[(o, pair)][:],
+            )
+
+        def store_v(g):
+            nc.sync.dma_start(
+                out=outs[V][g].rearrange("(c j) h d -> c (j h d)", j=SLABS), in_=staged[(g, V)][:]
             )
 
         grouped_we = new_grouped()
@@ -413,9 +418,11 @@ def tile_attention_pa_t_kernel(
                 vector_exit(Q, 2)
                 vector_exit(Q, 3)
                 store(g - 1, Q, 1)
-                store(g - 1, V, 0)
             v_low_exit(g - 1, 1)
-            store(g - 1, V, 1)
+            if g == 1:
+                store(0, V, 1)
+            else:
+                store_v(g - 1)
             if g > 1 and g < GROUPS:
                 k_bias_pair(1)
                 store(g - 1, K, 1)

@@ -74,19 +74,19 @@ def tile_attention_pa_t_kernel(
             )
 
         def load_bias(o):
-            nc.scalar.dma_start(
+            nc.sync.dma_start(
                 out=bias_rows[0:1, E * o : E * (o + 1)],
                 in_=biases[o].rearrange("(o n) -> o n", o=1),
             )
 
         load_halves(we_raw, we_view)
-        nc.scalar.dma_start(out=be_rows[0:1, :], in_=b_embed.rearrange("(o n) -> o n", o=1))
-        for o in (Q, K, V):
-            load_bias(o)
         load_halves(pos_raw, pos_view)
+        nc.sync.dma_start(out=be_rows[0:1, :], in_=b_embed.rearrange("(o n) -> o n", o=1))
         load_halves(x_raw[0], x_views[0])
         load_halves(w_raw[Q], weights[Q].rearrange("(m s) k -> m (s k)", s=SLABS))
         load_weight(K)
+        for o in (Q, K, V):
+            load_bias(o)
         load_weight(V)
         nc.sync.dma_start(out=x_raw[1][:], in_=x_views[1])
         for g in range(2, GROUPS):
@@ -106,6 +106,7 @@ def tile_attention_pa_t_kernel(
 
         fence = consts.tile([P, 1], U32)
         k_slabs = {}
+        spread = set()
         x_even_odd = {}
         pairs = {}
         x_mx = {}
@@ -124,7 +125,8 @@ def tile_attention_pa_t_kernel(
             return pairs[n]
 
         def spread_words(g, half):
-            if half == 0:
+            spread.add((g, half))
+            if g not in x_even_odd:
                 x_even_odd[g] = work.tile([P, 4 * E], BF16, tag="x_even_odd", name="x_even_odd", bufs=2)
             cols = slice(2 * E * half, 2 * E * (half + 1))
             nc.scalar.copy(
@@ -165,7 +167,7 @@ def tile_attention_pa_t_kernel(
 
         def turn_x(g):
             for half in range(2):
-                apart = g in x_even_odd
+                apart = (g, half) in spread
                 raw = x_even_odd[g] if apart else x_raw[g]
                 turn_half(raw, pair_of(g - 1)[:, 4 * E : 8 * E], half, False, nc.scalar.copy, apart)
 
@@ -292,11 +294,6 @@ def tile_attention_pa_t_kernel(
                 in_=staged_v(g, pair) if o == V else staged[(o, pair)][:],
             )
 
-        def store_v(g):
-            nc.sync.dma_start(
-                out=outs[V][g].rearrange("(c j) h d -> c (j h d)", j=SLABS), in_=staged[(g, V)][:]
-            )
-
         grouped_we = new_grouped()
         turn_half(we_raw, grouped_we[:], 0, False, nc.vector.tensor_copy, on_vec=True)
         turn_half(we_raw, grouped_we[:], 1, False, nc.scalar.copy)
@@ -377,6 +374,8 @@ def tile_attention_pa_t_kernel(
             vector_exit(Q, j)
             if j % 2 == 1:
                 store(0, Q, j // 2)
+        for half in range(2):
+            spread_words(2, half)
         turn_x(1)
         quantise(pair_of(0)[:, 4 * E : 8 * E], x_mx[1])
         nc.gpsimd.tensor_copy(out=fence[:], in_=x_mx[1][0][:, 0:1])
@@ -412,6 +411,7 @@ def tile_attention_pa_t_kernel(
             if g > 1:
                 v_high_back(g - 1, 0)
                 v_high_back(g - 1, 1)
+                store(g - 1, V, 0)
             if g + 2 < GROUPS:
                 turn_x(g + 2)
             if g > 1:
@@ -419,10 +419,7 @@ def tile_attention_pa_t_kernel(
                 vector_exit(Q, 3)
                 store(g - 1, Q, 1)
             v_low_exit(g - 1, 1)
-            if g == 1:
-                store(0, V, 1)
-            else:
-                store_v(g - 1)
+            store(g - 1, V, 1)
             if g > 1 and g < GROUPS:
                 k_bias_pair(1)
                 store(g - 1, K, 1)
@@ -457,8 +454,6 @@ def tile_attention_pa_t_kernel(
             next_stage1(2)
             v_high_pass(g, 1)
             v_high_bias(1)
-            if g + 3 < GROUPS:
-                spread_words(g + 3, 1)
             next_stage1(3)
             v_low_passes(g, 0)
             v_low_exit(g, 0)

from contextlib import ExitStack

import concourse.mybir as mybir
from concourse.masks import make_identity

F32 = mybir.dt.float32
BF16 = mybir.dt.bfloat16
U32 = mybir.dt.uint32
U8 = mybir.dt.uint8
I32 = mybir.dt.int32
FP8X4 = mybir.dt.float8_e4m3fn_x4
ADD = mybir.AluOpType.add
IDENTITY = mybir.ActivationFunctionType.Identity

P = 128
E = 512
H = E // 2
GROUPS = 8
SLABS = 4
Q, K, V = 0, 1, 2

FLOPS = 2 * GROUPS * SLABS * P * E * E * 4


def tile_attention_pa_t_kernel(
    tc, x, pos_embed, W_embed, b_embed, Wq, bq, Wk, bk, Wv, bv, out_0, out_1, out_2
):
    nc = tc.nc
    outs = [out_0, out_1, out_2]
    weights = [Wq, Wk, Wv]
    biases = [bq, bk, bv]
    with ExitStack() as ctx:
        consts = ctx.enter_context(tc.tile_pool(name="consts", bufs=1))
        raws = ctx.enter_context(tc.tile_pool(name="raws", bufs=1))
        work = ctx.enter_context(tc.tile_pool(name="work", bufs=2))
        stage = ctx.enter_context(tc.tile_pool(name="stage", bufs=7))
        vector_banks = ctx.enter_context(tc.psum_pool(name="vector_banks", bufs=4))
        scalar_banks = ctx.enter_context(tc.psum_pool(name="scalar_banks", bufs=4))
        ctx.enter_context(tc.manual_schedule())

        def vector_bank():
            return vector_banks.tile([P, E], F32, tag="vbank", name="vbank")

        def scalar_bank():
            return scalar_banks.tile([P, E], F32, tag="sbank", name="sbank")

        ident = consts.tile([P, P], F32)
        make_identity(nc, ident[:])
        be_rows = consts.tile([P, E], BF16)
        nc.vector.memset(be_rows[:].bitcast(I32), 0)
        ones = consts.tile([P, P], BF16)
        nc.vector.memset(ones[:], 1.0)
        bias_rows = consts.tile([P, 3 * E], BF16)
        nc.vector.memset(bias_rows[:].bitcast(I32), 0)
        warm = consts.tile([P, 1], F32)
        nc.scalar.activation(out=warm[:], in_=ones[:, 0:1], func=IDENTITY)

        we_raw = raws.tile([P, 4 * E], BF16)
        we_view = W_embed.rearrange("(m t) k -> m (t k)", t=4)
        x_raw = [raws.tile([P, 4 * E], BF16, name="x_raw%d" % g) for g in range(GROUPS)]
        x_views = [x[g].rearrange("(c j) a d -> c (j a d)", j=SLABS) for g in range(GROUPS)]
        pos_raw = raws.tile([P, 4 * E], BF16)
        pos_view = pos_embed.rearrange("(c j) e -> c (j e)", j=SLABS)
        w_raw = [raws.tile([P, 4 * E], BF16, name="w_raw%d" % o) for o in range(3)]

        def load_halves(dst, view):
            for half in range(2):
                cols = slice(2 * E * half, 2 * E * (half + 1))
                nc.sync.dma_start(out=dst[:, cols], in_=view[:, cols])

        def load_weight(o):
            nc.sync.dma_start(
                out=w_raw[o][:], in_=weights[o].rearrange("(m s) k -> m (s k)", s=SLABS)
            )

        def load_bias(o):
            nc.sync.dma_start(
                out=bias_rows[0:1, E * o : E * (o + 1)],
                in_=biases[o].rearrange("(o n) -> o n", o=1),
            )

        load_halves(we_raw, we_view)
        load_halves(pos_raw, pos_view)
        nc.sync.dma_start(out=be_rows[0:1, :], in_=b_embed.rearrange("(o n) -> o n", o=1))
        load_halves(x_raw[0], x_views[0])
        load_halves(w_raw[Q], weights[Q].rearrange("(m s) k -> m (s k)", s=SLABS))
        load_weight(K)
        for o in (Q, K, V):
            load_bias(o)
        load_weight(V)
        nc.sync.dma_start(out=x_raw[1][:], in_=x_views[1])
        for g in range(2, GROUPS):
            nc.sync.dma_start(out=x_raw[g][:], in_=x_views[g])

        def weight_mx(name):
            codes = consts.tile([P, E], U32, align_bytes=64, name=name + "_codes")
            scales = consts.tile([P, E], U8, align_bytes=64, name=name + "_scales")
            return (codes[:], scales[:])

        we_mx = weight_mx("we")
        w_mx = [weight_mx("w%d" % o) for o in range(3)]
        bias_all = consts.tile([P, 3 * E], BF16)
        be_col = consts.tile([P, 4], F32)
        bv_col = consts.tile([P, 2], F32)
        pos_t = consts.tile([P, 4 * E], F32)

        fence = consts.tile([P, 1], U32)
        k_slabs = {}
        spread = set()
        x_even_odd = {}
        pairs = {}
        x_mx = {}
        xe_mx = {}
        banks = {}
        staged = {}
        v_high = {}

        def new_grouped():
            grouped = work.tile([P, 4 * E], BF16, align_bytes=64, tag="grouped", bufs=4)
            return grouped

        def pair_of(n):
            if n not in pairs:
                pairs[n] = work.tile([P, 8 * E], BF16, align_bytes=64, tag="pair", name="pair")
            return pairs[n]

        def spread_words(g, half):
            spread.add((g, half))
            if g not in x_even_odd:
                x_even_odd[g] = work.tile([P, 4 * E], BF16, tag="x_even_odd", name="x_even_odd", bufs=2)
            cols = slice(2 * E * half, 2 * E * (half + 1))
            nc.scalar.copy(
                out=x_even_odd[g][:, cols].bitcast(F32).rearrange("p (s u m) -> p s u m", s=2, u=2),
                in_=x_raw[g][:, cols].bitcast(F32).rearrange("p (s m u) -> p s u m", s=2, u=2),
            )

        def turn_words(raw, half, new_bank, apart=False):
            words = raw[:].bitcast(F32)
            bank = new_bank()
            for s in range(2):
                start = H * (2 * half + s)
                for u in range(2):
                    if apart:
                        cols = slice(start + P * u, start + P * (u + 1))
                    else:
                        cols = slice(start + u, start + H, 2)
                    nc.tensor.transpose(bank[:, block(2 * s + u)], words[:, cols], ident[:])
            return bank

        def turn_half(raw, grouped, half, rows_interleaved, copy, apart=False, on_vec=False):
            bank = turn_words(raw, half, vector_bank if on_vec else scalar_bank, apart)
            gwords = grouped.bitcast(F32)
            if rows_interleaved:
                copy(
                    out=gwords.rearrange("p (m s u) -> p m s u", s=4, u=2)[
                        :, :, 2 * half : 2 * half + 2, :
                    ],
                    in_=bank[:].rearrange("p (s u m) -> p m s u", s=2, u=2),
                )
            else:
                copy(
                    out=gwords.rearrange("p (s m u) -> p s m u", s=4, u=2)[
                        :, 2 * half : 2 * half + 2, :, :
                    ],
                    in_=bank[:].rearrange("p (s u m) -> p s m u", s=2, u=2),
                )

        def turn_x(g):
            for half in range(2):
                apart = (g, half) in spread
                raw = x_even_odd[g] if apart else x_raw[g]
                turn_half(raw, pair_of(g - 1)[:, 4 * E : 8 * E], half, False, nc.scalar.copy, apart)

        def quantise(grouped, mx):
            nc.vector.quantize_mx(out=mx[0].bitcast(FP8X4), scales=mx[1], in_=grouped)

        def quantise_pair(n):
            codes = work.tile([P, 2 * E], U32, align_bytes=64, tag="codes", name="codes")
            scales = work.tile([P, 2 * E], U8, align_bytes=64, tag="scales", name="scales")
            first = 0 if n >= 0 else E
            last = 2 * E if n + 1 < GROUPS else E
            quantise(
                pair_of(n)[:, 4 * first : 4 * last], (codes[:, first:last], scales[:, first:last])
            )
            xe_mx[n] = (codes[:, 0:E], scales[:, 0:E])
            x_mx[n + 1] = (codes[:, E : 2 * E], scales[:, E : 2 * E])

        def mx_pass(out, stationary, s_cols, moving, m_cols):
            nc.tensor.matmul_mx(
                out=out,
                lhsT=stationary[0][:, s_cols].bitcast(FP8X4),
                lhsT_scale=stationary[1][:, s_cols],
                rhs=moving[0][:, m_cols].bitcast(FP8X4),
                rhs_scale=moving[1][:, m_cols],
                start=True,
                stop=True,
            )

        def block(i):
            return slice(P * i, P * (i + 1))

        def stage1_passes(g, j):
            bank = vector_bank()
            for t in range(4):
                mx_pass(bank[:, block(t)], we_mx, block(t), x_mx[g], block(j))
            banks[("s1", j)] = bank

        def stage1_exit(g, j):
            cols = slice(E * j, E * (j + 1))
            nc.vector.tensor_tensor(
                out=pair_of(g)[:, cols].rearrange("p (c t) -> p c t", t=4),
                in0=banks[("s1", j)][:].rearrange("p (t c) -> p c t", t=4),
                in1=pos_t[:, cols].rearrange("p (c t) -> p c t", t=4),
                op=ADD,
            )

        def staged_v(g, pair):
            if (g, V) not in staged:
                staged[(g, V)] = stage.tile([P, 4 * E], F32, name="st_v", tag="st_v", bufs=4)
            return staged[(g, V)][:, 2 * E * pair : 2 * E * (pair + 1)]

        def staged_slab(o, j):
            if j % 2 == 0:
                staged[(o, j // 2)] = stage.tile([P, 2 * E], F32, name="st%d" % o, tag="st%d" % o)
            return staged[(o, j // 2)][:, E * (j % 2) : E * (j % 2 + 1)]

        def full_pass(g, j, o, new_bank):
            banks[(o, j)] = new_bank()
            mx_pass(banks[(o, j)][:], xe_mx[g], block(j), w_mx[o], slice(0, E))

        def gpsimd_waits_for_quantise(n):
            nc.gpsimd.tensor_copy(out=fence[:], in_=xe_mx[n][0][:, 0:1])

        def vector_exit(o, j):
            nc.vector.tensor_tensor(
                out=staged_slab(o, j), in0=banks[(o, j)][:], in1=bias_all[:, E * o : E * (o + 1)], op=ADD
            )

        def k_copy(j):
            k_slabs[j] = staged_slab(K, j)
            nc.scalar.copy(out=k_slabs[j], in_=banks[(K, j)][:])

        def k_bias_pair(pair):
            both = staged[(K, pair)][:].rearrange("c (j e) -> c j e", j=2)
            nc.gpsimd.tensor_tensor(
                out=both,
                in0=both,
                in1=bias_all[:, E * K : E * (K + 1)].unsqueeze(1).to_broadcast([P, 2, E]),
                op=ADD,
            )

        def v_low_passes(g, pair):
            banks[(V, pair)] = vector_bank()
            for j2 in range(2):
                mx_pass(
                    banks[(V, pair)][:, H * j2 : H * (j2 + 1)], xe_mx[g], block(2 * pair + j2), w_mx[V], slice(0, H)
                )

        def v_low_exit(g, pair):
            nc.vector.tensor_tensor(
                out=staged_v(g, pair).rearrange("c (j e) -> c j e", j=2)[:, :, 0:H],
                in0=banks[(V, pair)][:].rearrange("c (j e) -> c j e", j=2),
                in1=bias_all[:, E * V : E * V + H].unsqueeze(1).to_broadcast([P, 2, H]),
                op=ADD,
            )

        def v_high_pass(g, i):
            banks[("vh", i)] = scalar_bank()
            mx_pass(banks[("vh", i)][:], w_mx[V], slice(H + P * i, H + P * (i + 1)), xe_mx[g], slice(0, E))

        def v_high_bias(i):
            v_high[i] = work.tile([P, E], F32, tag="v_high", name="v_high", bufs=4)
            nc.scalar.activation(
                out=v_high[i][:], in_=banks[("vh", i)][:], func=IDENTITY, bias=bv_col[:, i : i + 1]
            )

        def v_high_back(g, pair):
            bank = scalar_bank()
            for j2 in range(2):
                for i in range(2):
                    nc.tensor.transpose(
                        bank[:, block(2 * j2 + i)], v_high[i][:, block(2 * pair + j2)], ident[:]
                    )
            nc.scalar.copy(
                out=staged_v(g, pair).rearrange("c (j e) -> c j e", j=2)[:, :, H:E],
                in_=bank[:].rearrange("c (j e) -> c j e", j=2),
            )

        def store(g, o, pair):
            nc.sync.dma_start(
                out=outs[o][g].rearrange("(c j) h d -> c (j h d)", j=SLABS)[
                    :, 2 * E * pair : 2 * E * (pair + 1)
                ],
                in_=staged_v(g, pair) if o == V else staged[(o, pair)][:],
            )

        grouped_we = new_grouped()
        turn_half(we_raw, grouped_we[:], 0, False, nc.vector.tensor_copy, on_vec=True)
        turn_half(we_raw, grouped_we[:], 1, False, nc.scalar.copy)
        pos_banks = [turn_words(pos_raw, 0, vector_bank), turn_words(pos_raw, 1, vector_bank)]
        be_bank = scalar_bank()
        for u in range(2):
            nc.tensor.transpose(be_bank[:, block(u)], be_rows[:].bitcast(F32)[:, u:H:2], ident[:])
        nc.scalar.copy(
            out=be_col[:].rearrange("p (u e) -> p u e", u=2),
            in_=be_bank[:].bitcast(BF16).rearrange("p (u w) -> p u w", u=4)[:, 0:2, 0:2],
        )
        quantise(grouped_we[:], we_mx)
        for j in range(SLABS):
            nc.vector.tensor_tensor(
                out=pos_t[:, E * j : E * (j + 1)].rearrange("p (c u e) -> p c u e", u=2, e=2),
                in0=pos_banks[j // 2][:]
                .bitcast(BF16)
                .rearrange("p (s u c e) -> p s c u e", s=2, u=2, e=2)[:, j % 2],
                in1=be_col[:].rearrange("p (o u e) -> p o u e", o=1, u=2).to_broadcast([P, P, 2, 2]),
                op=ADD,
            )
        turn_x(0)
        quantise_pair(-1)
        grouped_w = {}

        def turn_weight(o):
            grouped_w[o] = new_grouped()
            for half in range(2):
                turn_half(w_raw[o], grouped_w[o][:], half, True, nc.scalar.copy)

        turn_weight(Q)
        turn_weight(K)
        for j in range(SLABS):
            stage1_passes(0, j)
        quantise(grouped_w[Q][:], w_mx[Q])
        for j in range(SLABS):
            stage1_exit(0, j)
        turn_weight(V)
        kq_bank = scalar_bank()
        v_bank = scalar_bank()
        for bank, o, place in ((kq_bank, Q, 0), (kq_bank, K, 1), (v_bank, V, 0)):
            nc.tensor.matmul(
                out=bank[:].bitcast(BF16)[:, E * place : E * (place + 1)],
                lhsT=ones[:],
                rhs=bias_rows[:, E * o : E * (o + 1)],
                start=True,
                stop=True,
            )
        bv_bank = scalar_bank()
        for i in range(2):
            first = E * V + H + P * i
            nc.tensor.matmul(
                out=bv_bank[:, 2 * i : 2 * i + 2],
                lhsT=bias_rows[:, first : first + P],
                rhs=ones[:, 0:2],
                start=True,
                stop=True,
            )
        nc.scalar.copy(out=bias_all[:, 0 : 2 * E], in_=kq_bank[:].bitcast(BF16))
        nc.scalar.copy(out=bias_all[:, 2 * E : 3 * E], in_=v_bank[:].bitcast(BF16)[:, 0:E])
        nc.scalar.copy(
            out=bv_col[:].unsqueeze(2), in_=bv_bank[:, 0:4].rearrange("p (i n) -> p i n", n=2)[:, :, 0:1]
        )

        def stage1_unit(g, j):
            stage1_passes(g, j)
            stage1_exit(g, j)

        first_codes = work.tile([P, 2 * E], U32, align_bytes=64, tag="codes", name="codes")
        first_scales = work.tile([P, 2 * E], U8, align_bytes=64, tag="scales", name="scales")
        xe_mx[0] = (first_codes[:, 0:E], first_scales[:, 0:E])
        x_mx[1] = (first_codes[:, E : 2 * E], first_scales[:, E : 2 * E])
        quantise(pair_of(0)[:, 0 : 4 * E], xe_mx[0])
        quantise(grouped_w[K][:], w_mx[K])
        quantise(grouped_w[V][:], w_mx[V])
        for j in range(SLABS):
            full_pass(0, j, Q, vector_bank)
            vector_exit(Q, j)
            if j % 2 == 1:
                store(0, Q, j // 2)
        for half in range(2):
            spread_words(2, half)
        turn_x(1)
        quantise(pair_of(0)[:, 4 * E : 8 * E], x_mx[1])
        nc.gpsimd.tensor_copy(out=fence[:], in_=x_mx[1][0][:, 0:1])
        for j in range(SLABS):
            full_pass(0, j, K, vector_bank if j < 2 else scalar_bank)
            if j < 2:
                vector_exit(K, j)
                if j == 1:
                    store(0, K, 0)
            else:
                k_copy(j)
        k_bias_pair(1)
        store(0, K, 1)
        for i in range(2):
            v_high_pass(0, i)
            v_high_bias(i)
        v_low_passes(0, 0)
        v_low_exit(0, 0)
        for j in range(2):
            stage1_unit(1, j)
        turn_x(2)
        for j in range(2, SLABS):
            stage1_unit(1, j)
        for pair in range(2):
            v_high_back(0, pair)
        store(0, V, 0)
        v_low_passes(0, 1)

        for g in range(1, GROUPS + 1):
            if g < GROUPS:
                quantise_pair(g)
                gpsimd_waits_for_quantise(g)
            if g > 1:
                v_high_back(g - 1, 0)
                v_high_back(g - 1, 1)
                store(g - 1, V, 0)
            if g + 2 < GROUPS:
                turn_x(g + 2)
            if g > 1:
                vector_exit(Q, 2)
                vector_exit(Q, 3)
                store(g - 1, Q, 1)
            v_low_exit(g - 1, 1)
            store(g - 1, V, 1)
            if g > 1 and g < GROUPS:
                k_bias_pair(1)
                store(g - 1, K, 1)
            if g == GROUPS:
                break

            def next_stage1(j):
                if g + 1 < GROUPS:
                    stage1_unit(g + 1, j)

            full_pass(g, 0, Q, vector_bank)
            vector_exit(Q, 0)
            for j in range(2):
                full_pass(g, j, K, vector_bank if g == GROUPS - 1 and j > 1 else scalar_bank)
                k_copy(j)
            k_bias_pair(0)
            next_stage1(0)
            full_pass(g, 1, Q, vector_bank)
            vector_exit(Q, 1)
            store(g, Q, 0)
            store(g, K, 0)
            next_stage1(1)
            if g == GROUPS - 1:
                for j in (2, 3):
                    full_pass(g, j, K, vector_bank if g == GROUPS - 1 and j > 1 else scalar_bank)
                    vector_exit(K, j)
                store(g, K, 1)
            if g + 3 < GROUPS:
                spread_words(g + 3, 0)
            v_high_pass(g, 0)
            v_high_bias(0)
            next_stage1(2)
            v_high_pass(g, 1)
            v_high_bias(1)
            next_stage1(3)
            v_low_passes(g, 0)
            v_low_exit(g, 0)
            if g < GROUPS - 1:
                for j in (2, 3):
                    full_pass(g, j, K, vector_bank if g == GROUPS - 1 and j > 1 else scalar_bank)
                    k_copy(j)
            for j in (2, 3):
                full_pass(g, j, Q, vector_bank)
            v_low_passes(g, 1)
